import numpy as np
import ml_dtypes


def mxq(x, axis, fmt="e4m3"):
    dtype, down = {"e4m3": (ml_dtypes.float8_e4m3fn, 7), "e5m2": (ml_dtypes.float8_e5m2, 14)}[fmt]
    v = np.moveaxis(np.asarray(x, np.float32).astype(ml_dtypes.bfloat16).astype(np.float64), axis, -1)
    blocks = v.reshape(v.shape[:-1] + (-1, 32))
    amax = np.abs(blocks).max(-1, keepdims=True)
    byte = np.maximum(np.where(amax > 0, np.frexp(amax)[1] - 1 + 127, 0) - down, 1)
    scale = np.exp2(byte - 127.0)
    codes = (blocks / scale).astype(np.float32).astype(dtype).astype(np.float64)
    return np.moveaxis((codes * scale).reshape(v.shape), -1, axis)


WIDE = False


def mx_kscale(k):
    if not WIDE:
        return np.ones(k)
    levels = np.array([10, -10, 5, -5, 0])
    a = np.random.permutation(np.resize(levels, k // 512 * 4)).reshape(k // 512, 4)
    idx = np.arange(k)
    return np.exp2(a[idx // 512, idx % 128 // 32])


BF16 = ml_dtypes.bfloat16


def bf(x):
    return np.asarray(x, np.float32).astype(BF16)


def f64(x):
    return np.asarray(x).astype(np.float64)


E2M1 = np.array([0.0, 0.5, 1.0, 1.5, 2.0, 3.0, 4.0, 6.0, -0.0, -0.5, -1.0, -1.5, -2.0, -3.0, -4.0, -6.0])


def pack_weight(w, fmt):
    k, n = w.shape
    w = f64(bf(w)).reshape(k // 32, 32, n)
    amax = np.abs(w).max(1)
    if fmt == "e4m3":
        byte = np.frexp(amax)[1] - 1 + 127 - 7
    else:
        mant, ex = np.frexp(amax / 6.0)
        byte = np.where(mant > 0.5, ex, ex - 1) + 127
    byte = np.clip(np.where(amax > 0, byte, 1), 1, 254)
    scaled = (w * np.exp2(127.0 - byte)[:, None, :]).reshape(k, n).astype(np.float32)
    by_word = np.ascontiguousarray(scaled.reshape(k // 512, 128, 4, n).transpose(0, 1, 3, 2))
    if fmt == "e4m3":
        words = by_word.astype(ml_dtypes.float8_e4m3fn).view(np.uint8)
    else:
        c = by_word.astype(ml_dtypes.float4_e2m1fn).view(np.uint8) & 0xF
        words = c[..., 0::2] | (c[..., 1::2] << 4)
    return np.ascontiguousarray(words), np.ascontiguousarray(byte.astype(np.uint8).reshape(k // 512, 16, n))


def unpack_weight(words, scales, fmt):
    g, p, n, _ = words.shape
    if fmt == "e4m3":
        vals = np.ascontiguousarray(words).view(ml_dtypes.float8_e4m3fn).astype(np.float64)
    else:
        nib = np.empty((g, p, n, 4), np.uint8)
        nib[..., 0::2] = words & 0xF
        nib[..., 1::2] = words >> 4
        vals = E2M1[nib]
    vals = vals * np.repeat(np.exp2(scales.astype(np.float64) - 127.0), 8, axis=1)[..., None]
    return vals.transpose(0, 1, 3, 2).reshape(g * 512, n)

def pack4(w):
    words, scales = pack_weight(w, "e2m1")
    return words.reshape(words.shape[0], 128, -1), scales


def unpack4(words, scales):
    return unpack_weight(words.reshape(words.shape[0], 128, -1, 2), scales, "e2m1")


B, I, H, ORDER = 1024, 512, 512, 3
MASK = 1.0 - 0.2


def sigmoid(v):
    return 1.0 / (1.0 + np.exp(-v))


def setup_inputs():
    s = mx_kscale(I)
    x = bf(np.random.standard_normal((B, I)) * s)
    h = bf(np.random.standard_normal((B, H)))
    c = bf(np.random.standard_normal((B, H)))
    mem_read = bf(np.random.standard_normal((B, H)) * 0.55)
    ih_words, ih_scales = pack4(np.random.standard_normal((I, 4 * H)) * 0.7 / np.sqrt(I) / s[:, None])
    hh_words, hh_scales = pack4(np.random.standard_normal((H, 4 * H)) * 0.7 / np.sqrt(H))
    bias = bf(np.random.standard_normal(4 * H) * 0.3)
    return {"x": x,
            "h": h,
            "c": c,
            "mem_read": mem_read,
            "W_ih_words": ih_words,
            "W_ih_scales": ih_scales,
            "W_hh_words": hh_words,
            "W_hh_scales": hh_scales,
            "bias": bias}


def reference(x, h, c, mem_read, W_ih_words, W_ih_scales, W_hh_words, W_hh_scales, bias):
    h0, c0 = f64(h), f64(c)
    gates = ((mxq(f64(x), 1, "e4m3") @ unpack4(W_ih_words, W_ih_scales))
             + (mxq(h0, 1, "e4m3") @ unpack4(W_hh_words, W_hh_scales))
             + f64(bias))
    f, i, o, g = np.split(gates, 4, axis=1)
    c_next = sigmoid(f) * c0 + sigmoid(i) * np.tanh(g) + f64(mem_read)
    h_next = sigmoid(o) * np.tanh(c_next)
    h_next = h_next * MASK + h0 * (1.0 - MASK)
    c_next = c_next * MASK + c0 * (1.0 - MASK)
    return h_next, c_next

@@ -1,0 +1,267 @@
+from contextlib import ExitStack
+
+import concourse.mybir as mybir
+from concourse.masks import make_identity
+
+F32 = mybir.dt.float32
+BF16 = mybir.dt.bfloat16
+I32 = mybir.dt.int32
+U32 = mybir.dt.uint32
+U8 = mybir.dt.uint8
+FP8X4 = mybir.dt.float8_e4m3fn_x4
+FP4X4 = mybir.dt.float4_e2m1fn_x4
+ACT = mybir.ActivationFunctionType
+ALU = mybir.AluOpType
+
+P = 128
+BATCH = 1024
+HIDDEN = 512
+K = 512
+PACK = 4
+K_WORDS = K // 2
+GATE_COLS = 4 * HIDDEN
+ROW_GROUPS = BATCH // P
+CHUNK = 512
+CHUNK_GROUPS = CHUNK // P
+N_CHUNKS = BATCH // CHUNK
+N_SLICES = HIDDEN // P
+GATE_F, GATE_I, GATE_O, GATE_G = 0, 1, 2, 3
+NEW_SHARE = 0.8
+OLD_SHARE = 0.2
+
+FLOPS = 2 * BATCH * (K + K) * GATE_COLS
+
+
+def load_rows(nc, pool, src, chunk, name):
+    rows = pool.tile([P, CHUNK_GROUPS, HIDDEN], BF16, name=name)
+    groups = slice(chunk * CHUNK_GROUPS, (chunk + 1) * CHUNK_GROUPS)
+    nc.sync.dma_start(out=rows[:], in_=src.rearrange("(r t) k -> r t k", t=ROW_GROUPS)[:, groups, :])
+    return rows
+
+
+def load_scale_rows(nc, plane, scales):
+    for quadrant in range(4):
+        nc.sync.dma_start(
+            out=plane[32 * quadrant : 32 * quadrant + 4, :].bitcast(I32),
+            in_=scales[0, 4 * quadrant : 4 * quadrant + 4, :].bitcast(I32),
+        )
+
+
+def regroup_for_quantize(nc, psum, rows, grouped, ident, copies):
+    words_out = (
+        grouped[:]
+        .rearrange("p n k -> p (n k)")
+        .bitcast(F32)
+        .rearrange("p (t r u) -> p t r u", t=CHUNK_GROUPS, u=2)
+    )
+    for pair in range(CHUNK_GROUPS // 2):
+        bank = psum.tile([P, 2, 2, P], F32, name="bank", tag="gate_bank")
+        for t in range(2):
+            words_in = rows[:, 2 * pair + t, :].bitcast(F32)
+            for u in range(2):
+                nc.tensor.transpose(bank[:, t, u, :], words_in[:, u:K_WORDS:2], ident[:])
+        copies[pair](
+            out=words_out[:, 2 * pair : 2 * pair + 2, :, :],
+            in_=bank[:].rearrange("p t u r -> p t r u"),
+        )
+
+
+def quantize(nc, grouped, codes, plane):
+    nc.vector.quantize_mx(
+        out=codes[:].bitcast(FP8X4),
+        scales=plane[:],
+        in_=grouped[:].rearrange("p n k -> p (n k)"),
+    )
+
+
+def turn_back(nc, psum, gate_t, ident, name):
+    back = psum.tile([P, CHUNK_GROUPS, P], F32, name=name, tag="back_bank")
+    for t in range(CHUNK_GROUPS):
+        nc.tensor.transpose(back[:, t, :], gate_t[:, t * P : (t + 1) * P], ident[:])
+    return back
+
+
+def tile_lstmcell_pb_kernel(
+    tc, x, h, c, mem_read, W_ih_words, W_ih_scales, W_hh_words, W_hh_scales, bias, out_0, out_1
+):
+    nc = tc.nc
+    h_next_rows = out_0.rearrange("(r t) n -> r t n", t=ROW_GROUPS)
+    c_next_rows = out_1.rearrange("(r t) n -> r t n", t=ROW_GROUPS)
+
+    with ExitStack() as stack:
+        keep = stack.enter_context(tc.tile_pool(name="keep", bufs=1))
+        gates_sb = stack.enter_context(tc.tile_pool(name="gates_sb", bufs=2))
+        work = stack.enter_context(tc.tile_pool(name="work", bufs=2))
+        outs = stack.enter_context(tc.tile_pool(name="outs", bufs=3))
+        gate_psum = stack.enter_context(tc.psum_pool(name="gate_psum", bufs=3))
+        back_psum = stack.enter_context(tc.psum_pool(name="back_psum", bufs=5))
+        stack.enter_context(tc.manual_schedule())
+
+        bias_rows = keep.tile([P, P], BF16, name="bias_rows")
+        nc.vector.memset(bias_rows[:], 0.0)
+        nc.scalar.dma_start(out=bias_rows[0 : GATE_COLS // P, :], in_=bias.rearrange("(a b) -> a b", b=P))
+
+        w_planes = []
+        for name in ("ih_plane", "hh_plane"):
+            plane = keep.tile([P, GATE_COLS], U8, name=name, align_bytes=64)
+            nc.vector.memset(plane[:].bitcast(I32), 0)
+            w_planes.append(plane)
+
+        warm_in = keep.tile([P, 1], F32, name="warm_in")
+        warm_out = keep.tile([P, 1], F32, name="warm_out")
+        nc.vector.memset(warm_in[:], 0.0)
+        nc.scalar.activation(out=warm_out[:], in_=warm_in[:], func=ACT.Sigmoid)
+
+        ident = keep.tile([P, P], F32, name="ident")
+        make_identity(nc, ident[:])
+
+        x_rows = [None, None]
+        h_rows = [None, None]
+        c_rows = [None, None]
+        m_rows = [None, None]
+        x_rows[0] = load_rows(nc, keep, x, 0, "x0")
+        h_rows[0] = load_rows(nc, keep, h, 0, "h0")
+        load_scale_rows(nc, w_planes[0], W_ih_scales)
+        load_scale_rows(nc, w_planes[1], W_hh_scales)
+        w_words = []
+        for name, words in (("ih_words", W_ih_words), ("hh_words", W_hh_words)):
+            packed = keep.tile([P, 2 * GATE_COLS], U8, name=name, align_bytes=64)
+            nc.sync.dma_start(out=packed[:].bitcast(I32), in_=words[0].bitcast(I32))
+            w_words.append(packed)
+        c_rows[0] = load_rows(nc, keep, c, 0, "c0")
+        m_rows[0] = load_rows(nc, keep, mem_read, 0, "m0")
+        x_rows[1] = load_rows(nc, keep, x, 1, "x1")
+        h_rows[1] = load_rows(nc, keep, h, 1, "h1")
+        c_rows[1] = load_rows(nc, keep, c, 1, "c1")
+        m_rows[1] = load_rows(nc, keep, mem_read, 1, "m1")
+
+        bias_wide = keep.tile([P, P], F32, name="bias_wide")
+        nc.vector.tensor_copy(out=bias_wide[:], in_=bias_rows[:])
+        bias_bank = gate_psum.tile([P, P], F32, name="bias_bank", tag="gate_bank")
+        nc.tensor.transpose(bias_bank[:], bias_wide[:], ident[:])
+        bias_cols = keep.tile([P, GATE_COLS // P], F32, name="bias_cols")
+        nc.vector.tensor_copy(out=bias_cols[:], in_=bias_bank[:, 0 : GATE_COLS // P])
+
+        grouped = {}
+        codes = {}
+        planes = {}
+        for operand in ("x", "h"):
+            for chunk in range(N_CHUNKS):
+                key = (operand, chunk)
+                tail = "_%s%d" % key
+                grouped[key] = keep.tile([P, CHUNK, PACK], BF16, name="grouped" + tail, align_bytes=64)
+                codes[key] = keep.tile([P, CHUNK], U32, name="codes" + tail, align_bytes=64)
+                planes[key] = keep.tile([P, CHUNK], U8, name="plane" + tail, align_bytes=64)
+        rows_of = {"x": x_rows, "h": h_rows}
+
+        for operand in ("x", "h"):
+            regroup_for_quantize(
+                nc, gate_psum, rows_of[operand][0], grouped[(operand, 0)], ident,
+                (nc.vector.tensor_copy, nc.scalar.copy),
+            )
+        for operand in ("x", "h"):
+            quantize(nc, grouped[(operand, 0)], codes[(operand, 0)], planes[(operand, 0)])
+
+        def hidden_product(unit_state):
+            h8 = work.tile([P, CHUNK_GROUPS, P], F32, name="h8")
+            nc.vector.scalar_tensor_tensor(
+                out=h8[:], in0=unit_state["o_back"][:], scalar=NEW_SHARE, in1=unit_state["tanh_cn"][:],
+                op0=ALU.mult, op1=ALU.mult,
+            )
+            return h8
+
+        def blend_and_store_hidden(unit_state, h8):
+            h_next = outs.tile([P, CHUNK_GROUPS, P], F32, name="h_next")
+            nc.vector.scalar_tensor_tensor(
+                out=h_next[:], in0=h_rows[unit_state["chunk"]][:, :, unit_state["cols"]], scalar=OLD_SHARE,
+                in1=h8[:], op0=ALU.mult, op1=ALU.add,
+            )
+            nc.sync.dma_start(out=h_next_rows[:, unit_state["groups"], unit_state["cols"]], in_=h_next[:])
+
+        def blend_and_store_cell(unit_state):
+            c_next = outs.tile([P, CHUNK_GROUPS, P], F32, name="c_next")
+            nc.vector.scalar_tensor_tensor(
+                out=c_next[:], in0=c_rows[unit_state["chunk"]][:, :, unit_state["cols"]], scalar=OLD_SHARE,
+                in1=unit_state["cn8"][:], op0=ALU.mult, op1=ALU.add,
+            )
+            nc.sync.dma_start(out=c_next_rows[:, unit_state["groups"], unit_state["cols"]], in_=c_next[:])
+
+        def tanh_of_cell(unit_state):
+            tanh_cn = work.tile([P, CHUNK_GROUPS, P], F32, name="tanh_cn")
+            nc.scalar.activation(out=tanh_cn[:], in_=unit_state["cn8"][:], func=ACT.Tanh, scale=1.0 / NEW_SHARE)
+            unit_state["tanh_cn"] = tanh_cn
+
+        before = None
+        for unit in range(N_CHUNKS * N_SLICES):
+            chunk, hidden_slice = divmod(unit, N_SLICES)
+            cols = slice(hidden_slice * P, (hidden_slice + 1) * P)
+            groups = slice(chunk * CHUNK_GROUPS, (chunk + 1) * CHUNK_GROUPS)
+
+            gate_t = {}
+            for gate in (GATE_I, GATE_G, GATE_F, GATE_O):
+                first_col = gate * HIDDEN + hidden_slice * P
+                acc = gate_psum.tile([P, CHUNK], F32, name="acc", tag="gate_bank")
+                for w, operand in enumerate(("x", "h")):
+                    nc.tensor.matmul_mx(
+                        out=acc[:],
+                        lhsT=w_words[w][:, 2 * first_col : 2 * (first_col + P)].bitcast(FP4X4),
+                        lhsT_scale=w_planes[w][:, first_col : first_col + P],
+                        rhs=codes[(operand, chunk)][:].bitcast(FP8X4),
+                        rhs_scale=planes[(operand, chunk)][:],
+                        start=(w == 0),
+                        stop=(w == 1),
+                    )
+                gate_t[gate] = gates_sb.tile([P, CHUNK], F32, name="gate_t%d" % gate)
+                nc.scalar.activation(
+                    out=gate_t[gate][:], in_=acc[:],
+                    func=(ACT.Tanh if gate == GATE_G else ACT.Sigmoid),
+                    bias=bias_cols[:, first_col // P : first_col // P + 1], scale=1.0,
+                )
+            if before is not None:
+                tanh_of_cell(before)
+
+            ig_t = gates_sb.tile([P, CHUNK], F32, name="ig_t")
+            nc.vector.scalar_tensor_tensor(
+                out=ig_t[:], in0=gate_t[GATE_I][:], scalar=NEW_SHARE, in1=gate_t[GATE_G][:],
+                op0=ALU.mult, op1=ALU.mult,
+            )
+            if before is not None:
+                blend_and_store_cell(before)
+
+            f_back = turn_back(nc, back_psum, gate_t[GATE_F], ident, "f_back")
+            o_back = turn_back(nc, back_psum, gate_t[GATE_O], ident, "o_back")
+            ig_back = turn_back(nc, back_psum, ig_t, ident, "ig_back")
+
+            ahead = None
+            if chunk + 1 < N_CHUNKS and hidden_slice in (1, 2):
+                ahead = ("x", "h")[hidden_slice - 1]
+            if ahead is not None:
+                regroup_for_quantize(
+                    nc, gate_psum, rows_of[ahead][chunk + 1], grouped[(ahead, chunk + 1)], ident,
+                    (nc.scalar.copy, nc.scalar.copy),
+                )
+
+            fc8 = work.tile([P, CHUNK_GROUPS, P], F32, name="fc8")
+            nc.vector.scalar_tensor_tensor(
+                out=fc8[:], in0=f_back[:], scalar=NEW_SHARE, in1=c_rows[chunk][:, :, cols],
+                op0=ALU.mult, op1=ALU.mult,
+            )
+            if before is not None:
+                h8 = hidden_product(before)
+            sum8 = work.tile([P, CHUNK_GROUPS, P], F32, name="sum8")
+            nc.vector.tensor_tensor(out=sum8[:], in0=ig_back[:], in1=fc8[:], op=ALU.add)
+            if before is not None:
+                blend_and_store_hidden(before, h8)
+            cn8 = work.tile([P, CHUNK_GROUPS, P], F32, name="cn8")
+            nc.vector.scalar_tensor_tensor(
+                out=cn8[:], in0=m_rows[chunk][:, :, cols], scalar=NEW_SHARE, in1=sum8[:],
+                op0=ALU.mult, op1=ALU.add,
+            )
+            if ahead is not None:
+                quantize(nc, grouped[(ahead, chunk + 1)], codes[(ahead, chunk + 1)], planes[(ahead, chunk + 1)])
+
+            before = {"chunk": chunk, "cols": cols, "groups": groups, "o_back": o_back, "cn8": cn8}
+
+        tanh_of_cell(before)
+        blend_and_store_cell(before)
+        blend_and_store_hidden(before, hidden_product(before))

@@ -119,15 +119,15 @@ def tile_lstmcell_pb_kernel(
         h_rows = [None, None]
         c_rows = [None, None]
         m_rows = [None, None]
+        w_words = []
+        for name in ("ih_words", "hh_words"):
+            w_words.append(keep.tile([P, 2 * GATE_COLS], U8, name=name, align_bytes=64))
         x_rows[0] = load_rows(nc, keep, x, 0, "x0")
         h_rows[0] = load_rows(nc, keep, h, 0, "h0")
         load_scale_rows(nc, w_planes[0], W_ih_scales)
+        nc.sync.dma_start(out=w_words[0][:].bitcast(I32), in_=W_ih_words[0].bitcast(I32))
+        nc.sync.dma_start(out=w_words[1][:].bitcast(I32), in_=W_hh_words[0].bitcast(I32))
         load_scale_rows(nc, w_planes[1], W_hh_scales)
-        w_words = []
-        for name, words in (("ih_words", W_ih_words), ("hh_words", W_hh_words)):
-            packed = keep.tile([P, 2 * GATE_COLS], U8, name=name, align_bytes=64)
-            nc.sync.dma_start(out=packed[:].bitcast(I32), in_=words[0].bitcast(I32))
-            w_words.append(packed)
         c_rows[0] = load_rows(nc, keep, c, 0, "c0")
         m_rows[0] = load_rows(nc, keep, mem_read, 0, "m0")
         x_rows[1] = load_rows(nc, keep, x, 1, "x1")
@@ -162,106 +162,115 @@ def tile_lstmcell_pb_kernel(
         for operand in ("x", "h"):
             quantize(nc, grouped[(operand, 0)], codes[(operand, 0)], planes[(operand, 0)])
 
-        def hidden_product(unit_state):
-            h8 = work.tile([P, CHUNK_GROUPS, P], F32, name="h8")
-            nc.vector.scalar_tensor_tensor(
-                out=h8[:], in0=unit_state["o_back"][:], scalar=NEW_SHARE, in1=unit_state["tanh_cn"][:],
-                op0=ALU.mult, op1=ALU.mult,
-            )
-            return h8
-
-        def blend_and_store_hidden(unit_state, h8):
-            h_next = outs.tile([P, CHUNK_GROUPS, P], F32, name="h_next")
-            nc.vector.scalar_tensor_tensor(
-                out=h_next[:], in0=h_rows[unit_state["chunk"]][:, :, unit_state["cols"]], scalar=OLD_SHARE,
-                in1=h8[:], op0=ALU.mult, op1=ALU.add,
-            )
-            nc.sync.dma_start(out=h_next_rows[:, unit_state["groups"], unit_state["cols"]], in_=h_next[:])
-
-        def blend_and_store_cell(unit_state):
-            c_next = outs.tile([P, CHUNK_GROUPS, P], F32, name="c_next")
-            nc.vector.scalar_tensor_tensor(
-                out=c_next[:], in0=c_rows[unit_state["chunk"]][:, :, unit_state["cols"]], scalar=OLD_SHARE,
-                in1=unit_state["cn8"][:], op0=ALU.mult, op1=ALU.add,
-            )
-            nc.sync.dma_start(out=c_next_rows[:, unit_state["groups"], unit_state["cols"]], in_=c_next[:])
-
-        def tanh_of_cell(unit_state):
-            tanh_cn = work.tile([P, CHUNK_GROUPS, P], F32, name="tanh_cn")
-            nc.scalar.activation(out=tanh_cn[:], in_=unit_state["cn8"][:], func=ACT.Tanh, scale=1.0 / NEW_SHARE)
-            unit_state["tanh_cn"] = tanh_cn
-
-        before = None
-        for unit in range(N_CHUNKS * N_SLICES):
+        n_units = N_CHUNKS * N_SLICES
+        units = []
+        for unit in range(n_units):
             chunk, hidden_slice = divmod(unit, N_SLICES)
-            cols = slice(hidden_slice * P, (hidden_slice + 1) * P)
-            groups = slice(chunk * CHUNK_GROUPS, (chunk + 1) * CHUNK_GROUPS)
+            units.append(
+                {
+                    "chunk": chunk,
+                    "hidden_slice": hidden_slice,
+                    "cols": slice(hidden_slice * P, (hidden_slice + 1) * P),
+                    "groups": slice(chunk * CHUNK_GROUPS, (chunk + 1) * CHUNK_GROUPS),
+                }
+            )
 
-            gate_t = {}
-            for gate in (GATE_I, GATE_G, GATE_F, GATE_O):
-                first_col = gate * HIDDEN + hidden_slice * P
-                acc = gate_psum.tile([P, CHUNK], F32, name="acc", tag="gate_bank")
-                for w, operand in enumerate(("x", "h")):
+        def two_gates(u, gates):
+            acc = {}
+            for gate in gates:
+                acc[gate] = gate_psum.tile([P, CHUNK], F32, name="acc", tag="gate_bank")
+            for w, operand in enumerate(("x", "h")):
+                for gate in gates:
+                    first_col = gate * HIDDEN + u["hidden_slice"] * P
                     nc.tensor.matmul_mx(
-                        out=acc[:],
+                        out=acc[gate][:],
                         lhsT=w_words[w][:, 2 * first_col : 2 * (first_col + P)].bitcast(FP4X4),
                         lhsT_scale=w_planes[w][:, first_col : first_col + P],
-                        rhs=codes[(operand, chunk)][:].bitcast(FP8X4),
-                        rhs_scale=planes[(operand, chunk)][:],
+                        rhs=codes[(operand, u["chunk"])][:].bitcast(FP8X4),
+                        rhs_scale=planes[(operand, u["chunk"])][:],
                         start=(w == 0),
                         stop=(w == 1),
                     )
-                gate_t[gate] = gates_sb.tile([P, CHUNK], F32, name="gate_t%d" % gate)
+            for gate in gates:
+                bias_col = gate * N_SLICES + u["hidden_slice"]
+                u[gate] = gates_sb.tile([P, CHUNK], F32, name="gate_t%d" % gate)
                 nc.scalar.activation(
-                    out=gate_t[gate][:], in_=acc[:],
+                    out=u[gate][:], in_=acc[gate][:],
                     func=(ACT.Tanh if gate == GATE_G else ACT.Sigmoid),
-                    bias=bias_cols[:, first_col // P : first_col // P + 1], scale=1.0,
+                    bias=bias_cols[:, bias_col : bias_col + 1], scale=1.0,
                 )
-            if before is not None:
-                tanh_of_cell(before)
 
-            ig_t = gates_sb.tile([P, CHUNK], F32, name="ig_t")
+        def input_times_candidate(u):
+            u["ig_t"] = gates_sb.tile([P, CHUNK], F32, name="ig_t")
             nc.vector.scalar_tensor_tensor(
-                out=ig_t[:], in0=gate_t[GATE_I][:], scalar=NEW_SHARE, in1=gate_t[GATE_G][:],
+                out=u["ig_t"][:], in0=u[GATE_I][:], scalar=NEW_SHARE, in1=u[GATE_G][:],
                 op0=ALU.mult, op1=ALU.mult,
             )
-            if before is not None:
-                blend_and_store_cell(before)
 
-            f_back = turn_back(nc, back_psum, gate_t[GATE_F], ident, "f_back")
-            o_back = turn_back(nc, back_psum, gate_t[GATE_O], ident, "o_back")
-            ig_back = turn_back(nc, back_psum, ig_t, ident, "ig_back")
+        def hidden_product(u):
+            u["h8"] = work.tile([P, CHUNK_GROUPS, P], F32, name="h8")
+            nc.vector.scalar_tensor_tensor(
+                out=u["h8"][:], in0=u["o_back"][:], scalar=NEW_SHARE, in1=u["tanh_cn"][:],
+                op0=ALU.mult, op1=ALU.mult,
+            )
+
+        def blend_and_store(u, old_rows, new8, out_rows, name):
+            blended = outs.tile([P, CHUNK_GROUPS, P], F32, name=name)
+            nc.vector.scalar_tensor_tensor(
+                out=blended[:], in0=old_rows[u["chunk"]][:, :, u["cols"]], scalar=OLD_SHARE, in1=new8[:],
+                op0=ALU.mult, op1=ALU.add,
+            )
+            nc.sync.dma_start(out=out_rows[:, u["groups"], u["cols"]], in_=blended[:])
+
+        two_gates(units[0], (GATE_I, GATE_G))
+        two_gates(units[0], (GATE_F, GATE_O))
+        input_times_candidate(units[0])
+
+        for n in range(n_units):
+            u = units[n]
+            after = units[n + 1] if n + 1 < n_units else None
+            before = units[n - 1] if n > 0 else None
+            chunk = u["chunk"]
+
+            if after is not None:
+                two_gates(after, (GATE_I, GATE_G))
+            f_back = turn_back(nc, back_psum, u[GATE_F], ident, "f_back")
+            u["o_back"] = turn_back(nc, back_psum, u[GATE_O], ident, "o_back")
+            ig_back = turn_back(nc, back_psum, u["ig_t"], ident, "ig_back")
 
             ahead = None
-            if chunk + 1 < N_CHUNKS and hidden_slice in (1, 2):
-                ahead = ("x", "h")[hidden_slice - 1]
-            if ahead is not None:
+            if chunk + 1 < N_CHUNKS and u["hidden_slice"] in (1, 2):
+                ahead = (("x", "h")[u["hidden_slice"] - 1], chunk + 1)
                 regroup_for_quantize(
-                    nc, gate_psum, rows_of[ahead][chunk + 1], grouped[(ahead, chunk + 1)], ident,
+                    nc, gate_psum, rows_of[ahead[0]][ahead[1]], grouped[ahead], ident,
                     (nc.scalar.copy, nc.scalar.copy),
                 )
+            if after is not None:
+                two_gates(after, (GATE_F, GATE_O))
 
             fc8 = work.tile([P, CHUNK_GROUPS, P], F32, name="fc8")
             nc.vector.scalar_tensor_tensor(
-                out=fc8[:], in0=f_back[:], scalar=NEW_SHARE, in1=c_rows[chunk][:, :, cols],
+                out=fc8[:], in0=f_back[:], scalar=NEW_SHARE, in1=c_rows[chunk][:, :, u["cols"]],
                 op0=ALU.mult, op1=ALU.mult,
             )
             if before is not None:
-                h8 = hidden_product(before)
+                hidden_product(before)
             sum8 = work.tile([P, CHUNK_GROUPS, P], F32, name="sum8")
             nc.vector.tensor_tensor(out=sum8[:], in0=ig_back[:], in1=fc8[:], op=ALU.add)
             if before is not None:
-                blend_and_store_hidden(before, h8)
+                blend_and_store(before, h_rows, before["h8"], h_next_rows, "h_next")
             cn8 = work.tile([P, CHUNK_GROUPS, P], F32, name="cn8")
             nc.vector.scalar_tensor_tensor(
-                out=cn8[:], in0=m_rows[chunk][:, :, cols], scalar=NEW_SHARE, in1=sum8[:],
+                out=cn8[:], in0=m_rows[chunk][:, :, u["cols"]], scalar=NEW_SHARE, in1=sum8[:],
                 op0=ALU.mult, op1=ALU.add,
             )
+            u["tanh_cn"] = work.tile([P, CHUNK_GROUPS, P], F32, name="tanh_cn")
+            nc.scalar.activation(out=u["tanh_cn"][:], in_=cn8[:], func=ACT.Tanh, scale=1.0 / NEW_SHARE)
+            if after is not None:
+                input_times_candidate(after)
             if ahead is not None:
-                quantize(nc, grouped[(ahead, chunk + 1)], codes[(ahead, chunk + 1)], planes[(ahead, chunk + 1)])
+                quantize(nc, grouped[ahead], codes[ahead], planes[ahead])
+            blend_and_store(u, c_rows, cn8, c_next_rows, "c_next")
 
-            before = {"chunk": chunk, "cols": cols, "groups": groups, "o_back": o_back, "cn8": cn8}
-
-        tanh_of_cell(before)
-        blend_and_store_cell(before)
-        blend_and_store_hidden(before, hidden_product(before))
+        hidden_product(units[-1])
+        blend_and_store(units[-1], h_rows, units[-1]["h8"], h_next_rows, "h_next")

@@ -135,13 +135,6 @@ def tile_lstmcell_pb_kernel(
         c_rows[1] = load_rows(nc, keep, c, 1, "c1")
         m_rows[1] = load_rows(nc, keep, mem_read, 1, "m1")
 
-        bias_wide = keep.tile([P, P], F32, name="bias_wide")
-        nc.vector.tensor_copy(out=bias_wide[:], in_=bias_rows[:])
-        bias_bank = gate_psum.tile([P, P], F32, name="bias_bank", tag="gate_bank")
-        nc.tensor.transpose(bias_bank[:], bias_wide[:], ident[:])
-        bias_cols = keep.tile([P, GATE_COLS // P], F32, name="bias_cols")
-        nc.vector.tensor_copy(out=bias_cols[:], in_=bias_bank[:, 0 : GATE_COLS // P])
-
         grouped = {}
         codes = {}
         planes = {}
@@ -154,13 +147,17 @@ def tile_lstmcell_pb_kernel(
                 planes[key] = keep.tile([P, CHUNK], U8, name="plane" + tail, align_bytes=64)
         rows_of = {"x": x_rows, "h": h_rows}
 
-        for operand in ("x", "h"):
-            regroup_for_quantize(
-                nc, gate_psum, rows_of[operand][0], grouped[(operand, 0)], ident,
-                (nc.vector.tensor_copy, nc.scalar.copy),
-            )
+        both_engines = (nc.vector.tensor_copy, nc.scalar.copy)
+        regroup_for_quantize(nc, gate_psum, x_rows[0], grouped[("x", 0)], ident, both_engines)
+        bias_wide = keep.tile([P, P], F32, name="bias_wide")
+        nc.vector.tensor_copy(out=bias_wide[:], in_=bias_rows[:])
+        regroup_for_quantize(nc, gate_psum, h_rows[0], grouped[("h", 0)], ident, both_engines)
+        bias_bank = gate_psum.tile([P, P], F32, name="bias_bank", tag="gate_bank")
+        nc.tensor.transpose(bias_bank[:], bias_wide[:], ident[:])
         for operand in ("x", "h"):
             quantize(nc, grouped[(operand, 0)], codes[(operand, 0)], planes[(operand, 0)])
+        bias_cols = keep.tile([P, GATE_COLS // P], F32, name="bias_cols")
+        nc.vector.tensor_copy(out=bias_cols[:], in_=bias_bank[:, 0 : GATE_COLS // P])
 
         n_units = N_CHUNKS * N_SLICES
         units = []
@@ -202,10 +199,37 @@ def tile_lstmcell_pb_kernel(
 
         def input_times_candidate(u):
             u["ig_t"] = gates_sb.tile([P, CHUNK], F32, name="ig_t")
+            nc.gpsimd.tensor_tensor(out=u["ig_t"][:], in0=u[GATE_I][:], in1=u[GATE_G][:], op=ALU.mult)
+
+        def old_cell_share(u):
+            u["c02"] = work.tile([P, CHUNK_GROUPS, P], F32, name="c02")
+            nc.scalar.mul(out=u["c02"][:], in_=c_rows[u["chunk"]][:, :, u["cols"]], mul=OLD_SHARE)
+
+        def forget_times_cell(u):
+            u["fc8"] = work.tile([P, CHUNK_GROUPS, P], F32, name="fc8")
             nc.vector.scalar_tensor_tensor(
-                out=u["ig_t"][:], in0=u[GATE_I][:], scalar=NEW_SHARE, in1=u[GATE_G][:],
+                out=u["fc8"][:], in0=u["f_back"][:], scalar=NEW_SHARE, in1=c_rows[u["chunk"]][:, :, u["cols"]],
                 op0=ALU.mult, op1=ALU.mult,
             )
+
+        def add_input_product(u):
+            u["sum8"] = work.tile([P, CHUNK_GROUPS, P], F32, name="sum8")
+            nc.vector.scalar_tensor_tensor(
+                out=u["sum8"][:], in0=u["ig_back"][:], scalar=NEW_SHARE, in1=u["fc8"][:],
+                op0=ALU.mult, op1=ALU.add,
+            )
+
+        def new_cell(u):
+            u["cn8"] = work.tile([P, CHUNK_GROUPS, P], F32, name="cn8")
+            nc.vector.scalar_tensor_tensor(
+                out=u["cn8"][:], in0=m_rows[u["chunk"]][:, :, u["cols"]], scalar=NEW_SHARE, in1=u["sum8"][:],
+                op0=ALU.mult, op1=ALU.add,
+            )
+            u["tanh_cn"] = work.tile([P, CHUNK_GROUPS, P], F32, name="tanh_cn")
+            nc.scalar.activation(out=u["tanh_cn"][:], in_=u["cn8"][:], func=ACT.Tanh, scale=1.0 / NEW_SHARE)
+            c_next = outs.tile([P, CHUNK_GROUPS, P], F32, name="c_next")
+            nc.gpsimd.tensor_tensor(out=c_next[:], in0=u["c02"][:], in1=u["cn8"][:], op=ALU.add)
+            nc.sync.dma_start(out=c_next_rows[:, u["groups"], u["cols"]], in_=c_next[:])
 
         def hidden_product(u):
             u["h8"] = work.tile([P, CHUNK_GROUPS, P], F32, name="h8")
@@ -214,29 +238,30 @@ def tile_lstmcell_pb_kernel(
                 op0=ALU.mult, op1=ALU.mult,
             )
 
-        def blend_and_store(u, old_rows, new8, out_rows, name):
-            blended = outs.tile([P, CHUNK_GROUPS, P], F32, name=name)
+        def new_hidden(u):
+            h_next = outs.tile([P, CHUNK_GROUPS, P], F32, name="h_next")
             nc.vector.scalar_tensor_tensor(
-                out=blended[:], in0=old_rows[u["chunk"]][:, :, u["cols"]], scalar=OLD_SHARE, in1=new8[:],
+                out=h_next[:], in0=h_rows[u["chunk"]][:, :, u["cols"]], scalar=OLD_SHARE, in1=u["h8"][:],
                 op0=ALU.mult, op1=ALU.add,
             )
-            nc.sync.dma_start(out=out_rows[:, u["groups"], u["cols"]], in_=blended[:])
+            nc.sync.dma_start(out=h_next_rows[:, u["groups"], u["cols"]], in_=h_next[:])
 
         two_gates(units[0], (GATE_I, GATE_G))
-        two_gates(units[0], (GATE_F, GATE_O))
         input_times_candidate(units[0])
+        two_gates(units[0], (GATE_F, GATE_O))
+        old_cell_share(units[0])
 
         for n in range(n_units):
             u = units[n]
             after = units[n + 1] if n + 1 < n_units else None
-            before = units[n - 1] if n > 0 else None
             chunk = u["chunk"]
 
             if after is not None:
                 two_gates(after, (GATE_I, GATE_G))
-            f_back = turn_back(nc, back_psum, u[GATE_F], ident, "f_back")
-            u["o_back"] = turn_back(nc, back_psum, u[GATE_O], ident, "o_back")
-            ig_back = turn_back(nc, back_psum, u["ig_t"], ident, "ig_back")
+                input_times_candidate(after)
+                old_cell_share(after)
+            u["f_back"] = turn_back(nc, back_psum, u[GATE_F], ident, "f_back")
+            u["ig_back"] = turn_back(nc, back_psum, u["ig_t"], ident, "ig_back")
 
             ahead = None
             if chunk + 1 < N_CHUNKS and u["hidden_slice"] in (1, 2):
@@ -247,30 +272,18 @@ def tile_lstmcell_pb_kernel(
                 )
             if after is not None:
                 two_gates(after, (GATE_F, GATE_O))
+            u["o_back"] = turn_back(nc, back_psum, u[GATE_O], ident, "o_back")
 
-            fc8 = work.tile([P, CHUNK_GROUPS, P], F32, name="fc8")
-            nc.vector.scalar_tensor_tensor(
-                out=fc8[:], in0=f_back[:], scalar=NEW_SHARE, in1=c_rows[chunk][:, :, u["cols"]],
-                op0=ALU.mult, op1=ALU.mult,
-            )
-            if before is not None:
-                hidden_product(before)
-            sum8 = work.tile([P, CHUNK_GROUPS, P], F32, name="sum8")
-            nc.vector.tensor_tensor(out=sum8[:], in0=ig_back[:], in1=fc8[:], op=ALU.add)
-            if before is not None:
-                blend_and_store(before, h_rows, before["h8"], h_next_rows, "h_next")
-            cn8 = work.tile([P, CHUNK_GROUPS, P], F32, name="cn8")
-            nc.vector.scalar_tensor_tensor(
-                out=cn8[:], in0=m_rows[chunk][:, :, u["cols"]], scalar=NEW_SHARE, in1=sum8[:],
-                op0=ALU.mult, op1=ALU.add,
-            )
-            u["tanh_cn"] = work.tile([P, CHUNK_GROUPS, P], F32, name="tanh_cn")
-            nc.scalar.activation(out=u["tanh_cn"][:], in_=cn8[:], func=ACT.Tanh, scale=1.0 / NEW_SHARE)
-            if after is not None:
-                input_times_candidate(after)
+            forget_times_cell(u)
+            if n >= 2:
+                new_hidden(units[n - 2])
+            add_input_product(u)
+            if n >= 1:
+                hidden_product(units[n - 1])
+            new_cell(u)
             if ahead is not None:
                 quantize(nc, grouped[ahead], codes[ahead], planes[ahead])
-            blend_and_store(u, c_rows, cn8, c_next_rows, "c_next")
 
+        new_hidden(units[-2])
         hidden_product(units[-1])
-        blend_and_store(units[-1], h_rows, units[-1]["h8"], h_next_rows, "h_next")
+        new_hidden(units[-1])

@@ -201,10 +201,6 @@ def tile_lstmcell_pb_kernel(
             u["ig_t"] = gates_sb.tile([P, CHUNK], F32, name="ig_t")
             nc.gpsimd.tensor_tensor(out=u["ig_t"][:], in0=u[GATE_I][:], in1=u[GATE_G][:], op=ALU.mult)
 
-        def old_cell_share(u):
-            u["c02"] = work.tile([P, CHUNK_GROUPS, P], F32, name="c02")
-            nc.scalar.mul(out=u["c02"][:], in_=c_rows[u["chunk"]][:, :, u["cols"]], mul=OLD_SHARE)
-
         def forget_times_cell(u):
             u["fc8"] = work.tile([P, CHUNK_GROUPS, P], F32, name="fc8")
             nc.vector.scalar_tensor_tensor(
@@ -227,8 +223,13 @@ def tile_lstmcell_pb_kernel(
             )
             u["tanh_cn"] = work.tile([P, CHUNK_GROUPS, P], F32, name="tanh_cn")
             nc.scalar.activation(out=u["tanh_cn"][:], in_=u["cn8"][:], func=ACT.Tanh, scale=1.0 / NEW_SHARE)
+
+        def new_cell_out(u):
             c_next = outs.tile([P, CHUNK_GROUPS, P], F32, name="c_next")
-            nc.gpsimd.tensor_tensor(out=c_next[:], in0=u["c02"][:], in1=u["cn8"][:], op=ALU.add)
+            nc.vector.scalar_tensor_tensor(
+                out=c_next[:], in0=c_rows[u["chunk"]][:, :, u["cols"]], scalar=OLD_SHARE, in1=u["cn8"][:],
+                op0=ALU.mult, op1=ALU.add,
+            )
             nc.sync.dma_start(out=c_next_rows[:, u["groups"], u["cols"]], in_=c_next[:])
 
         def hidden_product(u):
@@ -249,7 +250,6 @@ def tile_lstmcell_pb_kernel(
         two_gates(units[0], (GATE_I, GATE_G))
         input_times_candidate(units[0])
         two_gates(units[0], (GATE_F, GATE_O))
-        old_cell_share(units[0])
 
         for n in range(n_units):
             u = units[n]
@@ -259,7 +259,6 @@ def tile_lstmcell_pb_kernel(
             if after is not None:
                 two_gates(after, (GATE_I, GATE_G))
                 input_times_candidate(after)
-                old_cell_share(after)
             u["f_back"] = turn_back(nc, back_psum, u[GATE_F], ident, "f_back")
             u["ig_back"] = turn_back(nc, back_psum, u["ig_t"], ident, "ig_back")
 
@@ -275,15 +274,17 @@ def tile_lstmcell_pb_kernel(
             u["o_back"] = turn_back(nc, back_psum, u[GATE_O], ident, "o_back")
 
             forget_times_cell(u)
-            if n >= 2:
-                new_hidden(units[n - 2])
+            if n >= 1:
+                new_cell_out(units[n - 1])
             add_input_product(u)
             if n >= 1:
                 hidden_product(units[n - 1])
             new_cell(u)
+            if n >= 1:
+                new_hidden(units[n - 1])
             if ahead is not None:
                 quantize(nc, grouped[ahead], codes[ahead], planes[ahead])
 
-        new_hidden(units[-2])
+        new_cell_out(units[-1])
         hidden_product(units[-1])
         new_hidden(units[-1])

@@ -93,8 +93,8 @@ def tile_lstmcell_pb_kernel(
         gates_sb = stack.enter_context(tc.tile_pool(name="gates_sb", bufs=2))
         work = stack.enter_context(tc.tile_pool(name="work", bufs=2))
         outs = stack.enter_context(tc.tile_pool(name="outs", bufs=3))
-        gate_psum = stack.enter_context(tc.psum_pool(name="gate_psum", bufs=3))
-        back_psum = stack.enter_context(tc.psum_pool(name="back_psum", bufs=5))
+        gate_psum = stack.enter_context(tc.psum_pool(name="gate_psum", bufs=4))
+        back_psum = stack.enter_context(tc.psum_pool(name="back_psum", bufs=4))
         stack.enter_context(tc.manual_schedule())
 
         bias_rows = keep.tile([P, P], BF16, name="bias_rows")
@@ -172,27 +172,34 @@ def tile_lstmcell_pb_kernel(
                 }
             )
 
-        def two_gates(u, gates):
-            acc = {}
-            for gate in gates:
-                acc[gate] = gate_psum.tile([P, CHUNK], F32, name="acc", tag="gate_bank")
-            for w, operand in enumerate(("x", "h")):
+        def gate_sums(u):
+            if u["hidden_slice"] == 0:
+                gate_sets = ((GATE_I, GATE_G, GATE_F, GATE_O),)
+            else:
+                gate_sets = ((GATE_I, GATE_G), (GATE_F, GATE_O))
+            u["acc"] = {}
+            for gates in gate_sets:
                 for gate in gates:
-                    first_col = gate * HIDDEN + u["hidden_slice"] * P
-                    nc.tensor.matmul_mx(
-                        out=acc[gate][:],
-                        lhsT=w_words[w][:, 2 * first_col : 2 * (first_col + P)].bitcast(FP4X4),
-                        lhsT_scale=w_planes[w][:, first_col : first_col + P],
-                        rhs=codes[(operand, u["chunk"])][:].bitcast(FP8X4),
-                        rhs_scale=planes[(operand, u["chunk"])][:],
-                        start=(w == 0),
-                        stop=(w == 1),
-                    )
+                    u["acc"][gate] = gate_psum.tile([P, CHUNK], F32, name="acc", tag="gate_bank")
+                for w, operand in enumerate(("x", "h")):
+                    for gate in gates:
+                        first_col = gate * HIDDEN + u["hidden_slice"] * P
+                        nc.tensor.matmul_mx(
+                            out=u["acc"][gate][:],
+                            lhsT=w_words[w][:, 2 * first_col : 2 * (first_col + P)].bitcast(FP4X4),
+                            lhsT_scale=w_planes[w][:, first_col : first_col + P],
+                            rhs=codes[(operand, u["chunk"])][:].bitcast(FP8X4),
+                            rhs_scale=planes[(operand, u["chunk"])][:],
+                            start=(w == 0),
+                            stop=(w == 1),
+                        )
+
+        def activate(u, gates):
             for gate in gates:
                 bias_col = gate * N_SLICES + u["hidden_slice"]
                 u[gate] = gates_sb.tile([P, CHUNK], F32, name="gate_t%d" % gate)
                 nc.scalar.activation(
-                    out=u[gate][:], in_=acc[gate][:],
+                    out=u[gate][:], in_=u["acc"][gate][:],
                     func=(ACT.Tanh if gate == GATE_G else ACT.Sigmoid),
                     bias=bias_cols[:, bias_col : bias_col + 1], scale=1.0,
                 )
@@ -221,6 +228,8 @@ def tile_lstmcell_pb_kernel(
                 out=u["cn8"][:], in0=m_rows[u["chunk"]][:, :, u["cols"]], scalar=NEW_SHARE, in1=u["sum8"][:],
                 op0=ALU.mult, op1=ALU.add,
             )
+
+        def tanh_of_cell(u):
             u["tanh_cn"] = work.tile([P, CHUNK_GROUPS, P], F32, name="tanh_cn")
             nc.scalar.activation(out=u["tanh_cn"][:], in_=u["cn8"][:], func=ACT.Tanh, scale=1.0 / NEW_SHARE)
 
@@ -247,9 +256,10 @@ def tile_lstmcell_pb_kernel(
             )
             nc.sync.dma_start(out=h_next_rows[:, u["groups"], u["cols"]], in_=h_next[:])
 
-        two_gates(units[0], (GATE_I, GATE_G))
+        gate_sums(units[0])
+        activate(units[0], (GATE_I, GATE_G))
         input_times_candidate(units[0])
-        two_gates(units[0], (GATE_F, GATE_O))
+        activate(units[0], (GATE_F, GATE_O))
 
         for n in range(n_units):
             u = units[n]
@@ -257,10 +267,17 @@ def tile_lstmcell_pb_kernel(
             chunk = u["chunk"]
 
             if after is not None:
-                two_gates(after, (GATE_I, GATE_G))
+                gate_sums(after)
+                activate(after, (GATE_I, GATE_G))
                 input_times_candidate(after)
+                activate(after, (GATE_F,))
+            if n >= 1:
+                tanh_of_cell(units[n - 1])
+            if after is not None:
+                activate(after, (GATE_O,))
             u["f_back"] = turn_back(nc, back_psum, u[GATE_F], ident, "f_back")
             u["ig_back"] = turn_back(nc, back_psum, u["ig_t"], ident, "ig_back")
+            u["o_back"] = turn_back(nc, back_psum, u[GATE_O], ident, "o_back")
 
             ahead = None
             if chunk + 1 < N_CHUNKS and u["hidden_slice"] in (1, 2):
@@ -269,9 +286,6 @@ def tile_lstmcell_pb_kernel(
                     nc, gate_psum, rows_of[ahead[0]][ahead[1]], grouped[ahead], ident,
                     (nc.scalar.copy, nc.scalar.copy),
                 )
-            if after is not None:
-                two_gates(after, (GATE_F, GATE_O))
-            u["o_back"] = turn_back(nc, back_psum, u[GATE_O], ident, "o_back")
 
             forget_times_cell(u)
             if n >= 1:
@@ -285,6 +299,7 @@ def tile_lstmcell_pb_kernel(
             if ahead is not None:
                 quantize(nc, grouped[ahead], codes[ahead], planes[ahead])
 
+        tanh_of_cell(units[-1])
         new_cell_out(units[-1])
         hidden_product(units[-1])
         new_hidden(units[-1])

@@ -114,6 +114,8 @@ def tile_lstmcell_pb_kernel(
 
         ident = keep.tile([P, P], F32, name="ident")
         make_identity(nc, ident[:])
+        ident_bf16 = keep.tile([P, P], BF16, name="ident_bf16")
+        make_identity(nc, ident_bf16[:])
 
         x_rows = [None, None]
         h_rows = [None, None]
@@ -206,7 +208,19 @@ def tile_lstmcell_pb_kernel(
 
         def input_times_candidate(u):
             u["ig_t"] = gates_sb.tile([P, CHUNK], F32, name="ig_t")
-            nc.gpsimd.tensor_tensor(out=u["ig_t"][:], in0=u[GATE_I][:], in1=u[GATE_G][:], op=ALU.mult)
+            nc.vector.tensor_tensor(out=u["ig_t"][:], in0=u[GATE_I][:], in1=u[GATE_G][:], op=ALU.mult)
+
+        def input_plus_memory(u):
+            u["igm_back"] = back_psum.tile([P, CHUNK_GROUPS, P], F32, name="igm_back", tag="back_bank")
+            for t in range(CHUNK_GROUPS):
+                nc.tensor.matmul(
+                    out=u["igm_back"][:, t, :], lhsT=ident_bf16[:], rhs=m_rows[u["chunk"]][:, t, u["cols"]],
+                    start=True, stop=False,
+                )
+                nc.tensor.matmul(
+                    out=u["igm_back"][:, t, :], lhsT=u["ig_t"][:, t * P : (t + 1) * P], rhs=ident[:],
+                    is_transpose=True, start=False, stop=True,
+                )
 
         def forget_times_cell(u):
             u["fc8"] = work.tile([P, CHUNK_GROUPS, P], F32, name="fc8")
@@ -215,17 +229,10 @@ def tile_lstmcell_pb_kernel(
                 op0=ALU.mult, op1=ALU.mult,
             )
 
-        def add_input_product(u):
-            u["sum8"] = work.tile([P, CHUNK_GROUPS, P], F32, name="sum8")
-            nc.vector.scalar_tensor_tensor(
-                out=u["sum8"][:], in0=u["ig_back"][:], scalar=NEW_SHARE, in1=u["fc8"][:],
-                op0=ALU.mult, op1=ALU.add,
-            )
-
         def new_cell(u):
             u["cn8"] = work.tile([P, CHUNK_GROUPS, P], F32, name="cn8")
             nc.vector.scalar_tensor_tensor(
-                out=u["cn8"][:], in0=m_rows[u["chunk"]][:, :, u["cols"]], scalar=NEW_SHARE, in1=u["sum8"][:],
+                out=u["cn8"][:], in0=u["igm_back"][:], scalar=NEW_SHARE, in1=u["fc8"][:],
                 op0=ALU.mult, op1=ALU.add,
             )
 
@@ -257,9 +264,8 @@ def tile_lstmcell_pb_kernel(
             nc.sync.dma_start(out=h_next_rows[:, u["groups"], u["cols"]], in_=h_next[:])
 
         gate_sums(units[0])
-        activate(units[0], (GATE_I, GATE_G))
+        activate(units[0], (GATE_I, GATE_G, GATE_F, GATE_O))
         input_times_candidate(units[0])
-        activate(units[0], (GATE_F, GATE_O))
 
         for n in range(n_units):
             u = units[n]
@@ -268,15 +274,13 @@ def tile_lstmcell_pb_kernel(
 
             if after is not None:
                 gate_sums(after)
-                activate(after, (GATE_I, GATE_G))
-                input_times_candidate(after)
-                activate(after, (GATE_F,))
+                activate(after, (GATE_I, GATE_G, GATE_F))
             if n >= 1:
                 tanh_of_cell(units[n - 1])
             if after is not None:
                 activate(after, (GATE_O,))
             u["f_back"] = turn_back(nc, back_psum, u[GATE_F], ident, "f_back")
-            u["ig_back"] = turn_back(nc, back_psum, u["ig_t"], ident, "ig_back")
+            input_plus_memory(u)
             u["o_back"] = turn_back(nc, back_psum, u[GATE_O], ident, "o_back")
 
             ahead = None
@@ -287,19 +291,18 @@ def tile_lstmcell_pb_kernel(
                     (nc.scalar.copy, nc.scalar.copy),
                 )
 
+            if after is not None:
+                input_times_candidate(after)
             forget_times_cell(u)
-            if n >= 1:
-                new_cell_out(units[n - 1])
-            add_input_product(u)
             if n >= 1:
                 hidden_product(units[n - 1])
             new_cell(u)
             if n >= 1:
                 new_hidden(units[n - 1])
+            new_cell_out(u)
             if ahead is not None:
                 quantize(nc, grouped[ahead], codes[ahead], planes[ahead])
 
         tanh_of_cell(units[-1])
-        new_cell_out(units[-1])
         hidden_product(units[-1])
         new_hidden(units[-1])

@@ -32,10 +32,13 @@ OLD_SHARE = 0.2
 FLOPS = 2 * BATCH * (K + K) * GATE_COLS
 
 
-def load_rows(nc, pool, src, chunk, name):
+def load_rows(pool, src, chunk, name, start_dma, pieces=1):
     rows = pool.tile([P, CHUNK_GROUPS, HIDDEN], BF16, name=name)
-    groups = slice(chunk * CHUNK_GROUPS, (chunk + 1) * CHUNK_GROUPS)
-    nc.sync.dma_start(out=rows[:], in_=src.rearrange("(r t) k -> r t k", t=ROW_GROUPS)[:, groups, :])
+    by_group = src.rearrange("(r t) k -> r t k", t=ROW_GROUPS)
+    size = CHUNK_GROUPS // pieces
+    for t in range(0, CHUNK_GROUPS, size):
+        first = chunk * CHUNK_GROUPS + t
+        start_dma(out=rows[:, t : t + size, :], in_=by_group[:, first : first + size, :])
     return rows
 
 
@@ -48,30 +51,34 @@ def load_scale_rows(nc, plane, scales):
 
 
 def regroup_for_quantize(nc, psum, rows, grouped, ident, copies):
+    size = CHUNK_GROUPS // len(copies)
     words_out = (
         grouped[:]
         .rearrange("p n k -> p (n k)")
         .bitcast(F32)
         .rearrange("p (t r u) -> p t r u", t=CHUNK_GROUPS, u=2)
     )
-    for pair in range(CHUNK_GROUPS // 2):
-        bank = psum.tile([P, 2, 2, P], F32, name="bank", tag="gate_bank")
-        for t in range(2):
-            words_in = rows[:, 2 * pair + t, :].bitcast(F32)
+    for i, copy in enumerate(copies):
+        bank = psum.tile([P, size, 2, P], F32, name="bank", tag="gate_bank")
+        for t in range(size):
+            words_in = rows[:, size * i + t, :].bitcast(F32)
             for u in range(2):
                 nc.tensor.transpose(bank[:, t, u, :], words_in[:, u:K_WORDS:2], ident[:])
-        copies[pair](
-            out=words_out[:, 2 * pair : 2 * pair + 2, :, :],
+        copy(
+            out=words_out[:, size * i : size * (i + 1), :, :],
             in_=bank[:].rearrange("p t u r -> p t r u"),
         )
 
 
-def quantize(nc, grouped, codes, plane):
-    nc.vector.quantize_mx(
-        out=codes[:].bitcast(FP8X4),
-        scales=plane[:],
-        in_=grouped[:].rearrange("p n k -> p (n k)"),
-    )
+def quantize(nc, grouped, codes, plane, pieces=1):
+    size = CHUNK // pieces
+    for first in range(0, CHUNK, size):
+        rows = slice(first, first + size)
+        nc.vector.quantize_mx(
+            out=codes[:, rows].bitcast(FP8X4),
+            scales=plane[:, rows],
+            in_=grouped[:, rows, :].rearrange("p n k -> p (n k)"),
+        )
 
 
 def turn_back(nc, psum, gate_t, ident, name):
@@ -97,15 +104,26 @@ def tile_lstmcell_pb_kernel(
         back_psum = stack.enter_context(tc.psum_pool(name="back_psum", bufs=4))
         stack.enter_context(tc.manual_schedule())
 
-        bias_rows = keep.tile([P, P], BF16, name="bias_rows")
-        nc.vector.memset(bias_rows[:], 0.0)
-        nc.scalar.dma_start(out=bias_rows[0 : GATE_COLS // P, :], in_=bias.rearrange("(a b) -> a b", b=P))
-
         w_planes = []
         for name in ("ih_plane", "hh_plane"):
             plane = keep.tile([P, GATE_COLS], U8, name=name, align_bytes=64)
             nc.vector.memset(plane[:].bitcast(I32), 0)
             w_planes.append(plane)
+        bias_rows = keep.tile([P, P], BF16, name="bias_rows")
+        nc.gpsimd.memset(bias_rows[:], 0.0)
+        nc.gpsimd.dma_start(out=bias_rows[0 : GATE_COLS // P, :], in_=bias.rearrange("(a b) -> a b", b=P))
+
+        x_rows = [None, None]
+        h_rows = [None, None]
+        c_rows = [None, None]
+        m_rows = [None, None]
+        w_words = []
+        for name in ("ih_words", "hh_words"):
+            w_words.append(keep.tile([P, 2 * GATE_COLS], U8, name=name, align_bytes=64))
+        x_rows[0] = load_rows(keep, x, 0, "x0", nc.scalar.dma_start, pieces=2)
+        h_rows[0] = load_rows(keep, h, 0, "h0", nc.scalar.dma_start)
+        load_scale_rows(nc, w_planes[0], W_ih_scales)
+        nc.sync.dma_start(out=w_words[0][:].bitcast(I32), in_=W_ih_words[0].bitcast(I32))
 
         warm_in = keep.tile([P, 1], F32, name="warm_in")
         warm_out = keep.tile([P, 1], F32, name="warm_out")
@@ -117,25 +135,14 @@ def tile_lstmcell_pb_kernel(
         ident_bf16 = keep.tile([P, P], BF16, name="ident_bf16")
         make_identity(nc, ident_bf16[:])
 
-        x_rows = [None, None]
-        h_rows = [None, None]
-        c_rows = [None, None]
-        m_rows = [None, None]
-        w_words = []
-        for name in ("ih_words", "hh_words"):
-            w_words.append(keep.tile([P, 2 * GATE_COLS], U8, name=name, align_bytes=64))
-        x_rows[0] = load_rows(nc, keep, x, 0, "x0")
-        h_rows[0] = load_rows(nc, keep, h, 0, "h0")
-        load_scale_rows(nc, w_planes[0], W_ih_scales)
-        nc.sync.dma_start(out=w_words[0][:].bitcast(I32), in_=W_ih_words[0].bitcast(I32))
         nc.sync.dma_start(out=w_words[1][:].bitcast(I32), in_=W_hh_words[0].bitcast(I32))
         load_scale_rows(nc, w_planes[1], W_hh_scales)
-        c_rows[0] = load_rows(nc, keep, c, 0, "c0")
-        m_rows[0] = load_rows(nc, keep, mem_read, 0, "m0")
-        x_rows[1] = load_rows(nc, keep, x, 1, "x1")
-        h_rows[1] = load_rows(nc, keep, h, 1, "h1")
-        c_rows[1] = load_rows(nc, keep, c, 1, "c1")
-        m_rows[1] = load_rows(nc, keep, mem_read, 1, "m1")
+        c_rows[0] = load_rows(keep, c, 0, "c0", nc.sync.dma_start)
+        m_rows[0] = load_rows(keep, mem_read, 0, "m0", nc.sync.dma_start)
+        x_rows[1] = load_rows(keep, x, 1, "x1", nc.sync.dma_start)
+        h_rows[1] = load_rows(keep, h, 1, "h1", nc.sync.dma_start)
+        c_rows[1] = load_rows(keep, c, 1, "c1", nc.sync.dma_start)
+        m_rows[1] = load_rows(keep, mem_read, 1, "m1", nc.sync.dma_start)
 
         grouped = {}
         codes = {}
@@ -149,17 +156,15 @@ def tile_lstmcell_pb_kernel(
                 planes[key] = keep.tile([P, CHUNK], U8, name="plane" + tail, align_bytes=64)
         rows_of = {"x": x_rows, "h": h_rows}
 
-        both_engines = (nc.vector.tensor_copy, nc.scalar.copy)
-        regroup_for_quantize(nc, gate_psum, x_rows[0], grouped[("x", 0)], ident, both_engines)
-        bias_wide = keep.tile([P, P], F32, name="bias_wide")
-        nc.vector.tensor_copy(out=bias_wide[:], in_=bias_rows[:])
-        regroup_for_quantize(nc, gate_psum, h_rows[0], grouped[("h", 0)], ident, both_engines)
-        bias_bank = gate_psum.tile([P, P], F32, name="bias_bank", tag="gate_bank")
-        nc.tensor.transpose(bias_bank[:], bias_wide[:], ident[:])
+        in_turn = (nc.vector.tensor_copy, nc.scalar.copy) * (CHUNK_GROUPS // 2)
         for operand in ("x", "h"):
-            quantize(nc, grouped[(operand, 0)], codes[(operand, 0)], planes[(operand, 0)])
+            key = (operand, 0)
+            regroup_for_quantize(nc, gate_psum, rows_of[operand][0], grouped[key], ident, in_turn)
+            quantize(nc, grouped[key], codes[key], planes[key], pieces=2)
+        bias_bank = back_psum.tile([P, P], BF16, name="bias_bank", tag="back_bank")
+        nc.tensor.transpose(bias_bank[:], bias_rows[:], ident_bf16[:])
         bias_cols = keep.tile([P, GATE_COLS // P], F32, name="bias_cols")
-        nc.vector.tensor_copy(out=bias_cols[:], in_=bias_bank[:, 0 : GATE_COLS // P])
+        nc.scalar.copy(out=bias_cols[:], in_=bias_bank[:, 0 : GATE_COLS // P])
 
         n_units = N_CHUNKS * N_SLICES
         units = []

@@ -104,6 +104,18 @@ def tile_lstmcell_pb_kernel(
         back_psum = stack.enter_context(tc.psum_pool(name="back_psum", bufs=4))
         stack.enter_context(tc.manual_schedule())
 
+        warm_zeros = keep.tile([P, CHUNK], BF16, name="warm_zeros")
+        nc.vector.memset(warm_zeros[:], 0.0)
+        warm_bank = back_psum.tile([P, CHUNK], F32, name="warm_bank", tag="back_bank")
+
+        def keep_clock_up(n_matmuls):
+            for i in range(n_matmuls):
+                nc.tensor.matmul(
+                    out=warm_bank[:], lhsT=warm_zeros[:, 0:P], rhs=warm_zeros[:], start=True, stop=True
+                )
+
+        keep_clock_up(4)
+
         w_planes = []
         for name in ("ih_plane", "hh_plane"):
             plane = keep.tile([P, GATE_COLS], U8, name=name, align_bytes=64)
@@ -160,6 +172,8 @@ def tile_lstmcell_pb_kernel(
         for operand in ("x", "h"):
             key = (operand, 0)
             regroup_for_quantize(nc, gate_psum, rows_of[operand][0], grouped[key], ident, in_turn)
+            if operand == "x":
+                keep_clock_up(2)
             quantize(nc, grouped[key], codes[key], planes[key], pieces=2)
         bias_bank = back_psum.tile([P, P], BF16, name="bias_bank", tag="back_bank")
         nc.tensor.transpose(bias_bank[:], bias_rows[:], ident_bf16[:])
@@ -179,34 +193,28 @@ def tile_lstmcell_pb_kernel(
                 }
             )
 
-        def gate_sums(u):
-            if u["hidden_slice"] == 0:
-                gate_sets = ((GATE_I, GATE_G, GATE_F, GATE_O),)
-            else:
-                gate_sets = ((GATE_I, GATE_G), (GATE_F, GATE_O))
-            u["acc"] = {}
-            for gates in gate_sets:
+        def gate_sums(u, gates):
+            for gate in gates:
+                u["acc", gate] = gate_psum.tile([P, CHUNK], F32, name="acc", tag="gate_bank")
+            for w, operand in enumerate(("x", "h")):
                 for gate in gates:
-                    u["acc"][gate] = gate_psum.tile([P, CHUNK], F32, name="acc", tag="gate_bank")
-                for w, operand in enumerate(("x", "h")):
-                    for gate in gates:
-                        first_col = gate * HIDDEN + u["hidden_slice"] * P
-                        nc.tensor.matmul_mx(
-                            out=u["acc"][gate][:],
-                            lhsT=w_words[w][:, 2 * first_col : 2 * (first_col + P)].bitcast(FP4X4),
-                            lhsT_scale=w_planes[w][:, first_col : first_col + P],
-                            rhs=codes[(operand, u["chunk"])][:].bitcast(FP8X4),
-                            rhs_scale=planes[(operand, u["chunk"])][:],
-                            start=(w == 0),
-                            stop=(w == 1),
-                        )
+                    first_col = gate * HIDDEN + u["hidden_slice"] * P
+                    nc.tensor.matmul_mx(
+                        out=u["acc", gate][:],
+                        lhsT=w_words[w][:, 2 * first_col : 2 * (first_col + P)].bitcast(FP4X4),
+                        lhsT_scale=w_planes[w][:, first_col : first_col + P],
+                        rhs=codes[(operand, u["chunk"])][:].bitcast(FP8X4),
+                        rhs_scale=planes[(operand, u["chunk"])][:],
+                        start=(w == 0),
+                        stop=(w == 1),
+                    )
 
         def activate(u, gates):
             for gate in gates:
                 bias_col = gate * N_SLICES + u["hidden_slice"]
                 u[gate] = gates_sb.tile([P, CHUNK], F32, name="gate_t%d" % gate)
                 nc.scalar.activation(
-                    out=u[gate][:], in_=u["acc"][gate][:],
+                    out=u[gate][:], in_=u["acc", gate][:],
                     func=(ACT.Tanh if gate == GATE_G else ACT.Sigmoid),
                     bias=bias_cols[:, bias_col : bias_col + 1], scale=1.0,
                 )
@@ -268,8 +276,8 @@ def tile_lstmcell_pb_kernel(
             )
             nc.sync.dma_start(out=h_next_rows[:, u["groups"], u["cols"]], in_=h_next[:])
 
-        gate_sums(units[0])
-        activate(units[0], (GATE_I, GATE_G, GATE_F, GATE_O))
+        gate_sums(units[0], (GATE_I, GATE_G, GATE_F, GATE_O))
+        activate(units[0], (GATE_I, GATE_G))
         input_times_candidate(units[0])
 
         for n in range(n_units):
@@ -277,13 +285,16 @@ def tile_lstmcell_pb_kernel(
             after = units[n + 1] if n + 1 < n_units else None
             chunk = u["chunk"]
 
+            if n >= 1:
+                gate_sums(u, (GATE_F, GATE_O))
             if after is not None:
-                gate_sums(after)
-                activate(after, (GATE_I, GATE_G, GATE_F))
+                gate_sums(after, (GATE_I, GATE_G))
+            activate(u, (GATE_F,))
             if n >= 1:
                 tanh_of_cell(units[n - 1])
+            activate(u, (GATE_O,))
             if after is not None:
-                activate(after, (GATE_O,))
+                activate(after, (GATE_I, GATE_G))
             u["f_back"] = turn_back(nc, back_psum, u[GATE_F], ident, "f_back")
             input_plus_memory(u)
             u["o_back"] = turn_back(nc, back_psum, u[GATE_O], ident, "o_back")
@@ -296,12 +307,12 @@ def tile_lstmcell_pb_kernel(
                     (nc.scalar.copy, nc.scalar.copy),
                 )
 
-            if after is not None:
-                input_times_candidate(after)
             forget_times_cell(u)
             if n >= 1:
                 hidden_product(units[n - 1])
             new_cell(u)
+            if after is not None:
+                input_times_candidate(after)
             if n >= 1:
                 new_hidden(units[n - 1])
             new_cell_out(u)

@@ -223,16 +223,18 @@ def tile_lstmcell_pb_kernel(
             u["ig_t"] = gates_sb.tile([P, CHUNK], F32, name="ig_t")
             nc.vector.tensor_tensor(out=u["ig_t"][:], in0=u[GATE_I][:], in1=u[GATE_G][:], op=ALU.mult)
 
-        def input_plus_memory(u):
+        def lay_memory(u):
             u["igm_back"] = back_psum.tile([P, CHUNK_GROUPS, P], F32, name="igm_back", tag="back_bank")
+            nc.tensor.matmul(
+                out=u["igm_back"][:], lhsT=ident_bf16[:], rhs=m_rows[u["chunk"]][:, :, u["cols"]],
+                start=True, stop=False,
+            )
+
+        def add_input_product(u):
             for t in range(CHUNK_GROUPS):
                 nc.tensor.matmul(
-                    out=u["igm_back"][:, t, :], lhsT=ident_bf16[:], rhs=m_rows[u["chunk"]][:, t, u["cols"]],
-                    start=True, stop=False,
-                )
-                nc.tensor.matmul(
                     out=u["igm_back"][:, t, :], lhsT=u["ig_t"][:, t * P : (t + 1) * P], rhs=ident[:],
-                    is_transpose=True, start=False, stop=True,
+                    is_transpose=True, start=False, stop=(t == CHUNK_GROUPS - 1),
                 )
 
         def forget_times_cell(u):
@@ -295,8 +297,9 @@ def tile_lstmcell_pb_kernel(
             activate(u, (GATE_O,))
             if after is not None:
                 activate(after, (GATE_I, GATE_G))
+            lay_memory(u)
             u["f_back"] = turn_back(nc, back_psum, u[GATE_F], ident, "f_back")
-            input_plus_memory(u)
+            add_input_product(u)
             u["o_back"] = turn_back(nc, back_psum, u[GATE_O], ident, "o_back")
 
             ahead = None

@@ -244,16 +244,21 @@ def tile_lstmcell_pb_kernel(
                 op0=ALU.mult, op1=ALU.mult,
             )
 
-        def new_cell(u):
-            u["cn8"] = work.tile([P, CHUNK_GROUPS, P], F32, name="cn8")
+        all_groups = slice(0, CHUNK_GROUPS)
+        halves = (slice(0, CHUNK_GROUPS // 2), slice(CHUNK_GROUPS // 2, CHUNK_GROUPS))
+
+        def new_cell(u, part=all_groups):
+            if part.start == 0:
+                u["cn8"] = work.tile([P, CHUNK_GROUPS, P], F32, name="cn8")
             nc.vector.scalar_tensor_tensor(
-                out=u["cn8"][:], in0=u["igm_back"][:], scalar=NEW_SHARE, in1=u["fc8"][:],
+                out=u["cn8"][:, part, :], in0=u["igm_back"][:, part, :], scalar=NEW_SHARE, in1=u["fc8"][:, part, :],
                 op0=ALU.mult, op1=ALU.add,
             )
 
-        def tanh_of_cell(u):
-            u["tanh_cn"] = work.tile([P, CHUNK_GROUPS, P], F32, name="tanh_cn")
-            nc.scalar.activation(out=u["tanh_cn"][:], in_=u["cn8"][:], func=ACT.Tanh, scale=1.0 / NEW_SHARE)
+        def tanh_of_cell(u, part=all_groups):
+            if part.start == 0:
+                u["tanh_cn"] = work.tile([P, CHUNK_GROUPS, P], F32, name="tanh_cn")
+            nc.scalar.activation(out=u["tanh_cn"][:, part, :], in_=u["cn8"][:, part, :], func=ACT.Tanh, scale=1.0 / NEW_SHARE)
 
         def new_cell_out(u):
             c_next = outs.tile([P, CHUNK_GROUPS, P], F32, name="c_next")
@@ -263,20 +268,23 @@ def tile_lstmcell_pb_kernel(
             )
             nc.sync.dma_start(out=c_next_rows[:, u["groups"], u["cols"]], in_=c_next[:])
 
-        def hidden_product(u):
-            u["h8"] = work.tile([P, CHUNK_GROUPS, P], F32, name="h8")
+        def hidden_product(u, part=all_groups):
+            if part.start == 0:
+                u["h8"] = work.tile([P, CHUNK_GROUPS, P], F32, name="h8")
             nc.vector.scalar_tensor_tensor(
-                out=u["h8"][:], in0=u["o_back"][:], scalar=NEW_SHARE, in1=u["tanh_cn"][:],
+                out=u["h8"][:, part, :], in0=u["o_back"][:, part, :], scalar=NEW_SHARE, in1=u["tanh_cn"][:, part, :],
                 op0=ALU.mult, op1=ALU.mult,
             )
 
-        def new_hidden(u):
-            h_next = outs.tile([P, CHUNK_GROUPS, P], F32, name="h_next")
+        def new_hidden(u, part=all_groups):
+            n_groups = part.stop - part.start
+            first = u["chunk"] * CHUNK_GROUPS + part.start
+            h_next = outs.tile([P, n_groups, P], F32, name="h_next%d" % n_groups)
             nc.vector.scalar_tensor_tensor(
-                out=h_next[:], in0=h_rows[u["chunk"]][:, :, u["cols"]], scalar=OLD_SHARE, in1=u["h8"][:],
+                out=h_next[:], in0=h_rows[u["chunk"]][:, part, u["cols"]], scalar=OLD_SHARE, in1=u["h8"][:, part, :],
                 op0=ALU.mult, op1=ALU.add,
             )
-            nc.sync.dma_start(out=h_next_rows[:, u["groups"], u["cols"]], in_=h_next[:])
+            nc.sync.dma_start(out=h_next_rows[:, first : first + n_groups, u["cols"]], in_=h_next[:])
 
         gate_sums(units[0], (GATE_I, GATE_G, GATE_F, GATE_O))
         activate(units[0], (GATE_I, GATE_G))
@@ -288,7 +296,8 @@ def tile_lstmcell_pb_kernel(
             chunk = u["chunk"]
 
             if n >= 1:
-                gate_sums(u, (GATE_F, GATE_O))
+                gate_sums(u, (GATE_F,))
+                gate_sums(u, (GATE_O,))
             if after is not None:
                 gate_sums(after, (GATE_I, GATE_G))
             activate(u, (GATE_F,))
@@ -303,8 +312,8 @@ def tile_lstmcell_pb_kernel(
             u["o_back"] = turn_back(nc, back_psum, u[GATE_O], ident, "o_back")
 
             ahead = None
-            if chunk + 1 < N_CHUNKS and u["hidden_slice"] in (1, 2):
-                ahead = (("x", "h")[u["hidden_slice"] - 1], chunk + 1)
+            if chunk + 1 < N_CHUNKS and u["hidden_slice"] in (0, 1):
+                ahead = (("x", "h")[u["hidden_slice"]], chunk + 1)
                 regroup_for_quantize(
                     nc, gate_psum, rows_of[ahead[0]][ahead[1]], grouped[ahead], ident,
                     (nc.scalar.copy, nc.scalar.copy),
@@ -313,7 +322,9 @@ def tile_lstmcell_pb_kernel(
             forget_times_cell(u)
             if n >= 1:
                 hidden_product(units[n - 1])
-            new_cell(u)
+            parts = (all_groups,) if after is not None else halves
+            for part in parts:
+                new_cell(u, part)
             if after is not None:
                 input_times_candidate(after)
             if n >= 1:
@@ -322,6 +333,9 @@ def tile_lstmcell_pb_kernel(
             if ahead is not None:
                 quantize(nc, grouped[ahead], codes[ahead], planes[ahead])
 
-        tanh_of_cell(units[-1])
-        hidden_product(units[-1])
-        new_hidden(units[-1])
+        for part in halves:
+            tanh_of_cell(units[-1], part)
+        for part in halves:
+            hidden_product(units[-1], part)
+        for part in halves:
+            new_hidden(units[-1], part)

@@ -25,6 +25,8 @@ CHUNK = 512
 CHUNK_GROUPS = CHUNK // P
 N_CHUNKS = BATCH // CHUNK
 N_SLICES = HIDDEN // P
+W_PARTS = 2
+PART_COLS = HIDDEN // W_PARTS
 GATE_F, GATE_I, GATE_O, GATE_G = 0, 1, 2, 3
 NEW_SHARE = 0.8
 OLD_SHARE = 0.2
@@ -42,6 +44,14 @@ def load_rows(pool, src, chunk, name, start_dma, pieces=1):
     return rows
 
 
+def load_weight_words(nc, tile, words, part):
+    n = PART_COLS // 2
+    by_gate = words.bitcast(I32).rearrange("p (g n) -> p g n", g=4)
+    nc.sync.dma_start(
+        out=tile[:].bitcast(I32).rearrange("p (g n) -> p g n", g=4), in_=by_gate[:, :, part * n : (part + 1) * n]
+    )
+
+
 def load_scale_rows(nc, plane, scales):
     for quadrant in range(4):
         nc.sync.dma_start(
@@ -50,7 +60,15 @@ def load_scale_rows(nc, plane, scales):
         )
 
 
-def regroup_for_quantize(nc, psum, rows, grouped, ident, copies):
+def part_words(nc, rows, parted):
+    nc.vector.tensor_copy(
+        out=parted[:], in_=rows[:].rearrange("p t k -> p (t k)").bitcast(F32).rearrange(
+            "p (t w u) -> p t u w", t=CHUNK_GROUPS, u=2
+        )
+    )
+
+
+def regroup_for_quantize(nc, psum, words_in, grouped, ident, copies):
     size = CHUNK_GROUPS // len(copies)
     words_out = (
         grouped[:]
@@ -61,9 +79,8 @@ def regroup_for_quantize(nc, psum, rows, grouped, ident, copies):
     for i, copy in enumerate(copies):
         bank = psum.tile([P, size, 2, P], F32, name="bank", tag="gate_bank")
         for t in range(size):
-            words_in = rows[:, size * i + t, :].bitcast(F32)
             for u in range(2):
-                nc.tensor.transpose(bank[:, t, u, :], words_in[:, u:K_WORDS:2], ident[:])
+                nc.tensor.transpose(bank[:, t, u, :], words_in(size * i + t, u), ident[:])
         copy(
             out=words_out[:, size * i : size * (i + 1), :, :],
             in_=bank[:].rearrange("p t u r -> p t r u"),
@@ -131,11 +148,14 @@ def tile_lstmcell_pb_kernel(
         m_rows = [None, None]
         w_words = []
         for name in ("ih_words", "hh_words"):
-            w_words.append(keep.tile([P, 2 * GATE_COLS], U8, name=name, align_bytes=64))
+            tiles = []
+            for part in range(W_PARTS):
+                tiles.append(keep.tile([P, 2 * 4 * PART_COLS], U8, name=name + str(part), align_bytes=64))
+            w_words.append(tiles)
         x_rows[0] = load_rows(keep, x, 0, "x0", nc.scalar.dma_start, pieces=2)
         h_rows[0] = load_rows(keep, h, 0, "h0", nc.scalar.dma_start)
         load_scale_rows(nc, w_planes[0], W_ih_scales)
-        nc.sync.dma_start(out=w_words[0][:].bitcast(I32), in_=W_ih_words[0].bitcast(I32))
+        load_weight_words(nc, w_words[0][0], W_ih_words[0], 0)
 
         warm_in = keep.tile([P, 1], F32, name="warm_in")
         warm_out = keep.tile([P, 1], F32, name="warm_out")
@@ -147,11 +167,13 @@ def tile_lstmcell_pb_kernel(
         ident_bf16 = keep.tile([P, P], BF16, name="ident_bf16")
         make_identity(nc, ident_bf16[:])
 
-        nc.sync.dma_start(out=w_words[1][:].bitcast(I32), in_=W_hh_words[0].bitcast(I32))
+        load_weight_words(nc, w_words[1][0], W_hh_words[0], 0)
         load_scale_rows(nc, w_planes[1], W_hh_scales)
         c_rows[0] = load_rows(keep, c, 0, "c0", nc.sync.dma_start)
         m_rows[0] = load_rows(keep, mem_read, 0, "m0", nc.sync.dma_start)
         x_rows[1] = load_rows(keep, x, 1, "x1", nc.sync.dma_start)
+        load_weight_words(nc, w_words[0][1], W_ih_words[0], 1)
+        load_weight_words(nc, w_words[1][1], W_hh_words[0], 1)
         h_rows[1] = load_rows(keep, h, 1, "h1", nc.sync.dma_start)
         c_rows[1] = load_rows(keep, c, 1, "c1", nc.sync.dma_start)
         m_rows[1] = load_rows(keep, mem_read, 1, "m1", nc.sync.dma_start)
@@ -171,7 +193,10 @@ def tile_lstmcell_pb_kernel(
         in_turn = (nc.vector.tensor_copy, nc.scalar.copy) * (CHUNK_GROUPS // 2)
         for operand in ("x", "h"):
             key = (operand, 0)
-            regroup_for_quantize(nc, gate_psum, rows_of[operand][0], grouped[key], ident, in_turn)
+            rows = rows_of[operand][0]
+            regroup_for_quantize(
+                nc, gate_psum, lambda t, u: rows[:, t, :].bitcast(F32)[:, u:K_WORDS:2], grouped[key], ident, in_turn
+            )
             if operand == "x":
                 keep_clock_up(2)
             quantize(nc, grouped[key], codes[key], planes[key], pieces=2)
@@ -199,9 +224,11 @@ def tile_lstmcell_pb_kernel(
             for w, operand in enumerate(("x", "h")):
                 for gate in gates:
                     first_col = gate * HIDDEN + u["hidden_slice"] * P
+                    part, part_slice = divmod(u["hidden_slice"], PART_COLS // P)
+                    first_word = gate * PART_COLS + part_slice * P
                     nc.tensor.matmul_mx(
                         out=u["acc", gate][:],
-                        lhsT=w_words[w][:, 2 * first_col : 2 * (first_col + P)].bitcast(FP4X4),
+                        lhsT=w_words[w][part][:, 2 * first_word : 2 * (first_word + P)].bitcast(FP4X4),
                         lhsT_scale=w_planes[w][:, first_col : first_col + P],
                         rhs=codes[(operand, u["chunk"])][:].bitcast(FP8X4),
                         rhs_scale=planes[(operand, u["chunk"])][:],
@@ -289,6 +316,10 @@ def tile_lstmcell_pb_kernel(
         gate_sums(units[0], (GATE_I, GATE_G, GATE_F, GATE_O))
         activate(units[0], (GATE_I, GATE_G))
         input_times_candidate(units[0])
+        parted = {}
+        for operand in ("x", "h"):
+            parted[operand] = keep.tile([P, CHUNK_GROUPS, 2, P], F32, name="parted_" + operand)
+        part_words(nc, x_rows[1], parted["x"])
 
         for n in range(n_units):
             u = units[n]
@@ -312,14 +343,14 @@ def tile_lstmcell_pb_kernel(
             u["o_back"] = turn_back(nc, back_psum, u[GATE_O], ident, "o_back")
 
             ahead = None
+            forget_times_cell(u)
             if chunk + 1 < N_CHUNKS and u["hidden_slice"] in (0, 1):
                 ahead = (("x", "h")[u["hidden_slice"]], chunk + 1)
                 regroup_for_quantize(
-                    nc, gate_psum, rows_of[ahead[0]][ahead[1]], grouped[ahead], ident,
+                    nc, gate_psum, lambda t, u: parted[ahead[0]][:, t, u, :], grouped[ahead], ident,
                     (nc.scalar.copy, nc.scalar.copy),
                 )
 
-            forget_times_cell(u)
             if n >= 1:
                 hidden_product(units[n - 1])
             parts = (all_groups,) if after is not None else halves
@@ -332,6 +363,8 @@ def tile_lstmcell_pb_kernel(
             new_cell_out(u)
             if ahead is not None:
                 quantize(nc, grouped[ahead], codes[ahead], planes[ahead])
+            if n == 0:
+                part_words(nc, h_rows[1], parted["h"])
 
         for part in halves:
             tanh_of_cell(units[-1], part)

@@ -135,7 +135,7 @@ def tile_lstmcell_pb_kernel(
 
         w_planes = []
         for name in ("ih_plane", "hh_plane"):
-            plane = keep.tile([P, GATE_COLS], U8, name=name, align_bytes=64)
+            plane = keep.tile([P, GATE_COLS], U8, name=name, align_bytes=256)
             nc.vector.memset(plane[:].bitcast(I32), 0)
             w_planes.append(plane)
         bias_rows = keep.tile([P, P], BF16, name="bias_rows")
@@ -150,7 +150,7 @@ def tile_lstmcell_pb_kernel(
         for name in ("ih_words", "hh_words"):
             tiles = []
             for part in range(W_PARTS):
-                tiles.append(keep.tile([P, 2 * 4 * PART_COLS], U8, name=name + str(part), align_bytes=64))
+                tiles.append(keep.tile([P, 2 * 4 * PART_COLS], U8, name=name + str(part), align_bytes=256))
             w_words.append(tiles)
         x_rows[0] = load_rows(keep, x, 0, "x0", nc.scalar.dma_start, pieces=2)
         h_rows[0] = load_rows(keep, h, 0, "h0", nc.scalar.dma_start)
@@ -185,9 +185,9 @@ def tile_lstmcell_pb_kernel(
             for chunk in range(N_CHUNKS):
                 key = (operand, chunk)
                 tail = "_%s%d" % key
-                grouped[key] = keep.tile([P, CHUNK, PACK], BF16, name="grouped" + tail, align_bytes=64)
-                codes[key] = keep.tile([P, CHUNK], U32, name="codes" + tail, align_bytes=64)
-                planes[key] = keep.tile([P, CHUNK], U8, name="plane" + tail, align_bytes=64)
+                grouped[key] = keep.tile([P, CHUNK, PACK], BF16, name="grouped" + tail, align_bytes=256)
+                codes[key] = keep.tile([P, CHUNK], U32, name="codes" + tail, align_bytes=256)
+                planes[key] = keep.tile([P, CHUNK], U8, name="plane" + tail, align_bytes=256)
         rows_of = {"x": x_rows, "h": h_rows}
 
         in_turn = (nc.vector.tensor_copy, nc.scalar.copy) * (CHUNK_GROUPS // 2)

@@ -257,11 +257,11 @@ def tile_lstmcell_pb_kernel(
                 start=True, stop=False,
             )
 
-        def add_input_product(u):
+        def add_turned(u, product, closes=True):
             for t in range(CHUNK_GROUPS):
                 nc.tensor.matmul(
-                    out=u["igm_back"][:, t, :], lhsT=u["ig_t"][:, t * P : (t + 1) * P], rhs=ident[:],
-                    is_transpose=True, start=False, stop=(t == CHUNK_GROUPS - 1),
+                    out=u["igm_back"][:, t, :], lhsT=u[product][:, t * P : (t + 1) * P], rhs=ident[:],
+                    is_transpose=True, start=False, stop=(closes and t == CHUNK_GROUPS - 1),
                 )
 
         def forget_times_cell(u):
@@ -271,21 +271,16 @@ def tile_lstmcell_pb_kernel(
                 op0=ALU.mult, op1=ALU.mult,
             )
 
-        all_groups = slice(0, CHUNK_GROUPS)
-        halves = (slice(0, CHUNK_GROUPS // 2), slice(CHUNK_GROUPS // 2, CHUNK_GROUPS))
-
-        def new_cell(u, part=all_groups):
-            if part.start == 0:
-                u["cn8"] = work.tile([P, CHUNK_GROUPS, P], F32, name="cn8")
+        def new_cell(u):
+            u["cn8"] = work.tile([P, CHUNK_GROUPS, P], F32, name="cn8")
             nc.vector.scalar_tensor_tensor(
-                out=u["cn8"][:, part, :], in0=u["igm_back"][:, part, :], scalar=NEW_SHARE, in1=u["fc8"][:, part, :],
+                out=u["cn8"][:], in0=u["igm_back"][:], scalar=NEW_SHARE, in1=u["fc8"][:],
                 op0=ALU.mult, op1=ALU.add,
             )
 
-        def tanh_of_cell(u, part=all_groups):
-            if part.start == 0:
-                u["tanh_cn"] = work.tile([P, CHUNK_GROUPS, P], F32, name="tanh_cn")
-            nc.scalar.activation(out=u["tanh_cn"][:, part, :], in_=u["cn8"][:, part, :], func=ACT.Tanh, scale=1.0 / NEW_SHARE)
+        def tanh_of_cell(u):
+            u["tanh_cn"] = work.tile([P, CHUNK_GROUPS, P], F32, name="tanh_cn")
+            nc.scalar.activation(out=u["tanh_cn"][:], in_=u["cn8"][:], func=ACT.Tanh, scale=1.0 / NEW_SHARE)
 
         def new_cell_out(u):
             c_next = outs.tile([P, CHUNK_GROUPS, P], F32, name="c_next")
@@ -294,6 +289,37 @@ def tile_lstmcell_pb_kernel(
                 op0=ALU.mult, op1=ALU.add,
             )
             nc.sync.dma_start(out=c_next_rows[:, u["groups"], u["cols"]], in_=c_next[:])
+
+        def turn_cell(u):
+            u["c_t"] = back_psum.tile([P, CHUNK], BF16, name="c_t", tag="back_bank")
+            for t in range(CHUNK_GROUPS):
+                nc.tensor.transpose(
+                    u["c_t"][:, t * P : (t + 1) * P], c_rows[u["chunk"]][:, t, u["cols"]], ident_bf16[:]
+                )
+
+        def forget_times_cell_turned(u):
+            u["fc_t"] = gates_sb.tile([P, CHUNK], F32, name="fc_t")
+            nc.vector.tensor_tensor(out=u["fc_t"][:], in0=u[GATE_F][:], in1=u["c_t"][:], op=ALU.mult)
+
+        def old_cell_share(u):
+            u["c02"] = work.tile([P, CHUNK_GROUPS, P], F32, name="c02")
+            nc.scalar.mul(out=u["c02"][:], in_=c_rows[u["chunk"]][:, :, u["cols"]], mul=OLD_SHARE)
+
+        def tanh_of_sum(u, part):
+            if part.start == 0:
+                u["tanh_cn"] = work.tile([P, CHUNK_GROUPS, P], F32, name="tanh_cn")
+            nc.scalar.activation(out=u["tanh_cn"][:, part, :], in_=u["igm_back"][:, part, :], func=ACT.Tanh)
+
+        def cell_out_of_sum(u):
+            c_next = outs.tile([P, CHUNK_GROUPS, P], F32, name="c_next")
+            nc.vector.scalar_tensor_tensor(
+                out=c_next[:], in0=u["igm_back"][:], scalar=NEW_SHARE, in1=u["c02"][:],
+                op0=ALU.mult, op1=ALU.add,
+            )
+            nc.sync.dma_start(out=c_next_rows[:, u["groups"], u["cols"]], in_=c_next[:])
+
+        all_groups = slice(0, CHUNK_GROUPS)
+        halves = (slice(0, CHUNK_GROUPS // 2), slice(CHUNK_GROUPS // 2, CHUNK_GROUPS))
 
         def hidden_product(u, part=all_groups):
             if part.start == 0:
@@ -321,25 +347,22 @@ def tile_lstmcell_pb_kernel(
             parted[operand] = keep.tile([P, CHUNK_GROUPS, 2, P], F32, name="parted_" + operand)
         part_words(nc, x_rows[1], parted["x"])
 
-        for n in range(n_units):
+        for n in range(n_units - 1):
             u = units[n]
-            after = units[n + 1] if n + 1 < n_units else None
+            after = units[n + 1]
             chunk = u["chunk"]
 
             if n >= 1:
                 gate_sums(u, (GATE_F,))
                 gate_sums(u, (GATE_O,))
-            if after is not None:
-                gate_sums(after, (GATE_I, GATE_G))
-            activate(u, (GATE_F,))
+            gate_sums(after, (GATE_I, GATE_G))
+            activate(u, (GATE_F, GATE_O))
             if n >= 1:
                 tanh_of_cell(units[n - 1])
-            activate(u, (GATE_O,))
-            if after is not None:
-                activate(after, (GATE_I, GATE_G))
+            activate(after, (GATE_I, GATE_G))
             lay_memory(u)
             u["f_back"] = turn_back(nc, back_psum, u[GATE_F], ident, "f_back")
-            add_input_product(u)
+            add_turned(u, "ig_t")
             u["o_back"] = turn_back(nc, back_psum, u[GATE_O], ident, "o_back")
 
             ahead = None
@@ -353,22 +376,36 @@ def tile_lstmcell_pb_kernel(
 
             if n >= 1:
                 hidden_product(units[n - 1])
-            parts = (all_groups,) if after is not None else halves
-            for part in parts:
-                new_cell(u, part)
-            if after is not None:
-                input_times_candidate(after)
+            new_cell(u)
+            input_times_candidate(after)
             if n >= 1:
                 new_hidden(units[n - 1])
-            new_cell_out(u)
+            if n < n_units - 2:
+                new_cell_out(u)
             if ahead is not None:
                 quantize(nc, grouped[ahead], codes[ahead], planes[ahead])
             if n == 0:
                 part_words(nc, h_rows[1], parted["h"])
 
+        before, last = units[-2:]
+        gate_sums(last, (GATE_F,))
+        gate_sums(last, (GATE_O,))
+        old_cell_share(last)
+        activate(last, (GATE_F, GATE_O))
+        tanh_of_cell(before)
+        lay_memory(last)
+        turn_cell(last)
+        add_turned(last, "ig_t", closes=False)
+        last["o_back"] = turn_back(nc, back_psum, last[GATE_O], ident, "o_back")
+        forget_times_cell_turned(last)
+        add_turned(last, "fc_t")
+        hidden_product(before)
+        new_cell_out(before)
+        new_hidden(before)
         for part in halves:
-            tanh_of_cell(units[-1], part)
+            tanh_of_sum(last, part)
+        cell_out_of_sum(last)
         for part in halves:
-            hidden_product(units[-1], part)
+            hidden_product(last, part)
         for part in halves:
-            new_hidden(units[-1], part)
+            new_hidden(last, part)

from contextlib import ExitStack

import concourse.mybir as mybir
from concourse.masks import make_identity

F32 = mybir.dt.float32
BF16 = mybir.dt.bfloat16
I32 = mybir.dt.int32
U32 = mybir.dt.uint32
U8 = mybir.dt.uint8
FP8X4 = mybir.dt.float8_e4m3fn_x4
FP4X4 = mybir.dt.float4_e2m1fn_x4
ACT = mybir.ActivationFunctionType
ALU = mybir.AluOpType

P = 128
BATCH = 1024
HIDDEN = 512
K = 512
PACK = 4
K_WORDS = K // 2
GATE_COLS = 4 * HIDDEN
ROW_GROUPS = BATCH // P
CHUNK = 512
CHUNK_GROUPS = CHUNK // P
N_CHUNKS = BATCH // CHUNK
N_SLICES = HIDDEN // P
W_PARTS = 2
PART_COLS = HIDDEN // W_PARTS
GATE_F, GATE_I, GATE_O, GATE_G = 0, 1, 2, 3
NEW_SHARE = 0.8
OLD_SHARE = 0.2

FLOPS = 2 * BATCH * (K + K) * GATE_COLS


def load_rows(pool, src, chunk, name, start_dma, pieces=1):
    rows = pool.tile([P, CHUNK_GROUPS, HIDDEN], BF16, name=name)
    by_group = src.rearrange("(r t) k -> r t k", t=ROW_GROUPS)
    size = CHUNK_GROUPS // pieces
    for t in range(0, CHUNK_GROUPS, size):
        first = chunk * CHUNK_GROUPS + t
        start_dma(out=rows[:, t : t + size, :], in_=by_group[:, first : first + size, :])
    return rows


def load_weight_words(nc, tile, words, part):
    n = PART_COLS // 2
    by_gate = words.bitcast(I32).rearrange("p (g n) -> p g n", g=4)
    nc.sync.dma_start(
        out=tile[:].bitcast(I32).rearrange("p (g n) -> p g n", g=4), in_=by_gate[:, :, part * n : (part + 1) * n]
    )


def load_scale_rows(nc, plane, scales):
    for quadrant in range(4):
        nc.sync.dma_start(
            out=plane[32 * quadrant : 32 * quadrant + 4, :].bitcast(I32),
            in_=scales[0, 4 * quadrant : 4 * quadrant + 4, :].bitcast(I32),
        )


def part_words(nc, rows, parted):
    nc.vector.tensor_copy(
        out=parted[:], in_=rows[:].rearrange("p t k -> p (t k)").bitcast(F32).rearrange(
            "p (t w u) -> p t u w", t=CHUNK_GROUPS, u=2
        )
    )


def regroup_for_quantize(nc, psum, words_in, grouped, ident, copies):
    size = CHUNK_GROUPS // len(copies)
    words_out = (
        grouped[:]
        .rearrange("p n k -> p (n k)")
        .bitcast(F32)
        .rearrange("p (t r u) -> p t r u", t=CHUNK_GROUPS, u=2)
    )
    for i, copy in enumerate(copies):
        bank = psum.tile([P, size, 2, P], F32, name="bank", tag="gate_bank")
        for t in range(size):
            for u in range(2):
                nc.tensor.transpose(bank[:, t, u, :], words_in(size * i + t, u), ident[:])
        copy(
            out=words_out[:, size * i : size * (i + 1), :, :],
            in_=bank[:].rearrange("p t u r -> p t r u"),
        )


def quantize(nc, grouped, codes, plane, pieces=1):
    size = CHUNK // pieces
    for first in range(0, CHUNK, size):
        rows = slice(first, first + size)
        nc.vector.quantize_mx(
            out=codes[:, rows].bitcast(FP8X4),
            scales=plane[:, rows],
            in_=grouped[:, rows, :].rearrange("p n k -> p (n k)"),
        )


def turn_back(nc, psum, gate_t, ident, name):
    back = psum.tile([P, CHUNK_GROUPS, P], F32, name=name, tag="back_bank")
    for t in range(CHUNK_GROUPS):
        nc.tensor.transpose(back[:, t, :], gate_t[:, t * P : (t + 1) * P], ident[:])
    return back


def tile_lstmcell_pb_kernel(
    tc, x, h, c, mem_read, W_ih_words, W_ih_scales, W_hh_words, W_hh_scales, bias, out_0, out_1
):
    nc = tc.nc
    h_next_rows = out_0.rearrange("(r t) n -> r t n", t=ROW_GROUPS)
    c_next_rows = out_1.rearrange("(r t) n -> r t n", t=ROW_GROUPS)

    with ExitStack() as stack:
        keep = stack.enter_context(tc.tile_pool(name="keep", bufs=1))
        gates_sb = stack.enter_context(tc.tile_pool(name="gates_sb", bufs=2))
        work = stack.enter_context(tc.tile_pool(name="work", bufs=2))
        outs = stack.enter_context(tc.tile_pool(name="outs", bufs=3))
        gate_psum = stack.enter_context(tc.psum_pool(name="gate_psum", bufs=4))
        back_psum = stack.enter_context(tc.psum_pool(name="back_psum", bufs=4))
        stack.enter_context(tc.manual_schedule())

        warm_zeros = keep.tile([P, CHUNK], BF16, name="warm_zeros")
        nc.vector.memset(warm_zeros[:], 0.0)
        warm_bank = back_psum.tile([P, CHUNK], F32, name="warm_bank", tag="back_bank")

        def keep_clock_up(n_matmuls):
            for i in range(n_matmuls):
                nc.tensor.matmul(
                    out=warm_bank[:], lhsT=warm_zeros[:, 0:P], rhs=warm_zeros[:], start=True, stop=True
                )

        keep_clock_up(4)

        w_planes = []
        for name in ("ih_plane", "hh_plane"):
            plane = keep.tile([P, GATE_COLS], U8, name=name, align_bytes=256)
            nc.vector.memset(plane[:].bitcast(I32), 0)
            w_planes.append(plane)
        bias_rows = keep.tile([P, P], BF16, name="bias_rows")
        nc.gpsimd.memset(bias_rows[:], 0.0)
        nc.gpsimd.dma_start(out=bias_rows[0 : GATE_COLS // P, :], in_=bias.rearrange("(a b) -> a b", b=P))

        x_rows = [None, None]
        h_rows = [None, None]
        c_rows = [None, None]
        m_rows = [None, None]
        w_words = []
        for name in ("ih_words", "hh_words"):
            tiles = []
            for part in range(W_PARTS):
                tiles.append(keep.tile([P, 2 * 4 * PART_COLS], U8, name=name + str(part), align_bytes=256))
            w_words.append(tiles)
        x_rows[0] = load_rows(keep, x, 0, "x0", nc.scalar.dma_start, pieces=2)
        h_rows[0] = load_rows(keep, h, 0, "h0", nc.scalar.dma_start)
        load_scale_rows(nc, w_planes[0], W_ih_scales)
        load_weight_words(nc, w_words[0][0], W_ih_words[0], 0)

        warm_in = keep.tile([P, 1], F32, name="warm_in")
        warm_out = keep.tile([P, 1], F32, name="warm_out")
        nc.vector.memset(warm_in[:], 0.0)
        nc.scalar.activation(out=warm_out[:], in_=warm_in[:], func=ACT.Sigmoid)

        ident = keep.tile([P, P], F32, name="ident")
        make_identity(nc, ident[:])
        ident_bf16 = keep.tile([P, P], BF16, name="ident_bf16")
        make_identity(nc, ident_bf16[:])

        load_weight_words(nc, w_words[1][0], W_hh_words[0], 0)
        load_scale_rows(nc, w_planes[1], W_hh_scales)
        c_rows[0] = load_rows(keep, c, 0, "c0", nc.sync.dma_start)
        m_rows[0] = load_rows(keep, mem_read, 0, "m0", nc.sync.dma_start)
        x_rows[1] = load_rows(keep, x, 1, "x1", nc.sync.dma_start)
        load_weight_words(nc, w_words[0][1], W_ih_words[0], 1)
        load_weight_words(nc, w_words[1][1], W_hh_words[0], 1)
        h_rows[1] = load_rows(keep, h, 1, "h1", nc.sync.dma_start)
        c_rows[1] = load_rows(keep, c, 1, "c1", nc.sync.dma_start)
        m_rows[1] = load_rows(keep, mem_read, 1, "m1", nc.sync.dma_start)

        grouped = {}
        codes = {}
        planes = {}
        for operand in ("x", "h"):
            for chunk in range(N_CHUNKS):
                key = (operand, chunk)
                tail = "_%s%d" % key
                grouped[key] = keep.tile([P, CHUNK, PACK], BF16, name="grouped" + tail, align_bytes=256)
                codes[key] = keep.tile([P, CHUNK], U32, name="codes" + tail, align_bytes=256)
                planes[key] = keep.tile([P, CHUNK], U8, name="plane" + tail, align_bytes=256)
        rows_of = {"x": x_rows, "h": h_rows}

        in_turn = (nc.vector.tensor_copy, nc.scalar.copy) * (CHUNK_GROUPS // 2)
        for operand in ("x", "h"):
            key = (operand, 0)
            rows = rows_of[operand][0]
            regroup_for_quantize(
                nc, gate_psum, lambda t, u: rows[:, t, :].bitcast(F32)[:, u:K_WORDS:2], grouped[key], ident, in_turn
            )
            if operand == "x":
                keep_clock_up(2)
            quantize(nc, grouped[key], codes[key], planes[key], pieces=2)
        bias_bank = back_psum.tile([P, P], BF16, name="bias_bank", tag="back_bank")
        nc.tensor.transpose(bias_bank[:], bias_rows[:], ident_bf16[:])
        bias_cols = keep.tile([P, GATE_COLS // P], F32, name="bias_cols")
        nc.scalar.copy(out=bias_cols[:], in_=bias_bank[:, 0 : GATE_COLS // P])

        n_units = N_CHUNKS * N_SLICES
        units = []
        for unit in range(n_units):
            chunk, hidden_slice = divmod(unit, N_SLICES)
            units.append(
                {
                    "chunk": chunk,
                    "hidden_slice": hidden_slice,
                    "cols": slice(hidden_slice * P, (hidden_slice + 1) * P),
                    "groups": slice(chunk * CHUNK_GROUPS, (chunk + 1) * CHUNK_GROUPS),
                }
            )

        def gate_sums(u, gates):
            for gate in gates:
                u["acc", gate] = gate_psum.tile([P, CHUNK], F32, name="acc", tag="gate_bank")
            for w, operand in enumerate(("x", "h")):
                for gate in gates:
                    first_col = gate * HIDDEN + u["hidden_slice"] * P
                    part, part_slice = divmod(u["hidden_slice"], PART_COLS // P)
                    first_word = gate * PART_COLS + part_slice * P
                    nc.tensor.matmul_mx(
                        out=u["acc", gate][:],
                        lhsT=w_words[w][part][:, 2 * first_word : 2 * (first_word + P)].bitcast(FP4X4),
                        lhsT_scale=w_planes[w][:, first_col : first_col + P],
                        rhs=codes[(operand, u["chunk"])][:].bitcast(FP8X4),
                        rhs_scale=planes[(operand, u["chunk"])][:],
                        start=(w == 0),
                        stop=(w == 1),
                    )

        def activate(u, gates):
            for gate in gates:
                bias_col = gate * N_SLICES + u["hidden_slice"]
                u[gate] = gates_sb.tile([P, CHUNK], F32, name="gate_t%d" % gate)
                nc.scalar.activation(
                    out=u[gate][:], in_=u["acc", gate][:],
                    func=(ACT.Tanh if gate == GATE_G else ACT.Sigmoid),
                    bias=bias_cols[:, bias_col : bias_col + 1], scale=1.0,
                )

        def input_times_candidate(u):
            u["ig_t"] = gates_sb.tile([P, CHUNK], F32, name="ig_t")
            nc.vector.tensor_tensor(out=u["ig_t"][:], in0=u[GATE_I][:], in1=u[GATE_G][:], op=ALU.mult)

        def lay_memory(u):
            u["igm_back"] = back_psum.tile([P, CHUNK_GROUPS, P], F32, name="igm_back", tag="back_bank")
            nc.tensor.matmul(
                out=u["igm_back"][:], lhsT=ident_bf16[:], rhs=m_rows[u["chunk"]][:, :, u["cols"]],
                start=True, stop=False,
            )

        def add_turned(u, product, closes=True):
            for t in range(CHUNK_GROUPS):
                nc.tensor.matmul(
                    out=u["igm_back"][:, t, :], lhsT=u[product][:, t * P : (t + 1) * P], rhs=ident[:],
                    is_transpose=True, start=False, stop=(closes and t == CHUNK_GROUPS - 1),
                )

        def forget_times_cell(u):
            u["fc8"] = work.tile([P, CHUNK_GROUPS, P], F32, name="fc8")
            nc.vector.scalar_tensor_tensor(
                out=u["fc8"][:], in0=u["f_back"][:], scalar=NEW_SHARE, in1=c_rows[u["chunk"]][:, :, u["cols"]],
                op0=ALU.mult, op1=ALU.mult,
            )

        def new_cell(u):
            u["cn8"] = work.tile([P, CHUNK_GROUPS, P], F32, name="cn8")
            nc.vector.scalar_tensor_tensor(
                out=u["cn8"][:], in0=u["igm_back"][:], scalar=NEW_SHARE, in1=u["fc8"][:],
                op0=ALU.mult, op1=ALU.add,
            )

        def tanh_of_cell(u):
            u["tanh_cn"] = work.tile([P, CHUNK_GROUPS, P], F32, name="tanh_cn")
            nc.scalar.activation(out=u["tanh_cn"][:], in_=u["cn8"][:], func=ACT.Tanh, scale=1.0 / NEW_SHARE)

        def new_cell_out(u):
            c_next = outs.tile([P, CHUNK_GROUPS, P], F32, name="c_next")
            nc.vector.scalar_tensor_tensor(
                out=c_next[:], in0=c_rows[u["chunk"]][:, :, u["cols"]], scalar=OLD_SHARE, in1=u["cn8"][:],
                op0=ALU.mult, op1=ALU.add,
            )
            nc.sync.dma_start(out=c_next_rows[:, u["groups"], u["cols"]], in_=c_next[:])

        def turn_cell(u):
            u["c_t"] = back_psum.tile([P, CHUNK], BF16, name="c_t", tag="back_bank")
            for t in range(CHUNK_GROUPS):
                nc.tensor.transpose(
                    u["c_t"][:, t * P : (t + 1) * P], c_rows[u["chunk"]][:, t, u["cols"]], ident_bf16[:]
                )

        def forget_times_cell_turned(u):
            u["fc_t"] = gates_sb.tile([P, CHUNK], F32, name="fc_t")
            nc.vector.tensor_tensor(out=u["fc_t"][:], in0=u[GATE_F][:], in1=u["c_t"][:], op=ALU.mult)

        def old_cell_share(u):
            u["c02"] = work.tile([P, CHUNK_GROUPS, P], F32, name="c02")
            nc.scalar.mul(out=u["c02"][:], in_=c_rows[u["chunk"]][:, :, u["cols"]], mul=OLD_SHARE)

        def tanh_of_sum(u, part):
            if part.start == 0:
                u["tanh_cn"] = work.tile([P, CHUNK_GROUPS, P], F32, name="tanh_cn")
            nc.scalar.activation(out=u["tanh_cn"][:, part, :], in_=u["igm_back"][:, part, :], func=ACT.Tanh)

        def cell_out_of_sum(u):
            c_next = outs.tile([P, CHUNK_GROUPS, P], F32, name="c_next")
            nc.vector.scalar_tensor_tensor(
                out=c_next[:], in0=u["igm_back"][:], scalar=NEW_SHARE, in1=u["c02"][:],
                op0=ALU.mult, op1=ALU.add,
            )
            nc.sync.dma_start(out=c_next_rows[:, u["groups"], u["cols"]], in_=c_next[:])

        all_groups = slice(0, CHUNK_GROUPS)
        halves = (slice(0, CHUNK_GROUPS // 2), slice(CHUNK_GROUPS // 2, CHUNK_GROUPS))

        def hidden_product(u, part=all_groups):
            if part.start == 0:
                u["h8"] = work.tile([P, CHUNK_GROUPS, P], F32, name="h8")
            nc.vector.scalar_tensor_tensor(
                out=u["h8"][:, part, :], in0=u["o_back"][:, part, :], scalar=NEW_SHARE, in1=u["tanh_cn"][:, part, :],
                op0=ALU.mult, op1=ALU.mult,
            )

        def new_hidden(u, part=all_groups):
            n_groups = part.stop - part.start
            first = u["chunk"] * CHUNK_GROUPS + part.start
            h_next = outs.tile([P, n_groups, P], F32, name="h_next%d" % n_groups)
            nc.vector.scalar_tensor_tensor(
                out=h_next[:], in0=h_rows[u["chunk"]][:, part, u["cols"]], scalar=OLD_SHARE, in1=u["h8"][:, part, :],
                op0=ALU.mult, op1=ALU.add,
            )
            nc.sync.dma_start(out=h_next_rows[:, first : first + n_groups, u["cols"]], in_=h_next[:])

        gate_sums(units[0], (GATE_I, GATE_G, GATE_F, GATE_O))
        activate(units[0], (GATE_I, GATE_G))
        input_times_candidate(units[0])
        parted = {}
        for operand in ("x", "h"):
            parted[operand] = keep.tile([P, CHUNK_GROUPS, 2, P], F32, name="parted_" + operand)
        part_words(nc, x_rows[1], parted["x"])

        for n in range(n_units - 1):
            u = units[n]
            after = units[n + 1]
            chunk = u["chunk"]

            if n >= 1:
                gate_sums(u, (GATE_F,))
                gate_sums(u, (GATE_O,))
            gate_sums(after, (GATE_I, GATE_G))
            activate(u, (GATE_F, GATE_O))
            if n >= 1:
                tanh_of_cell(units[n - 1])
            activate(after, (GATE_I, GATE_G))
            lay_memory(u)
            u["f_back"] = turn_back(nc, back_psum, u[GATE_F], ident, "f_back")
            add_turned(u, "ig_t")
            u["o_back"] = turn_back(nc, back_psum, u[GATE_O], ident, "o_back")

            ahead = None
            forget_times_cell(u)
            if chunk + 1 < N_CHUNKS and u["hidden_slice"] in (0, 1):
                ahead = (("x", "h")[u["hidden_slice"]], chunk + 1)
                regroup_for_quantize(
                    nc, gate_psum, lambda t, u: parted[ahead[0]][:, t, u, :], grouped[ahead], ident,
                    (nc.scalar.copy, nc.scalar.copy),
                )

            if n >= 1:
                hidden_product(units[n - 1])
            new_cell(u)
            input_times_candidate(after)
            if n >= 1:
                new_hidden(units[n - 1])
            if n < n_units - 2:
                new_cell_out(u)
            if ahead is not None:
                quantize(nc, grouped[ahead], codes[ahead], planes[ahead])
            if n == 0:
                part_words(nc, h_rows[1], parted["h"])

        before, last = units[-2:]
        gate_sums(last, (GATE_F,))
        gate_sums(last, (GATE_O,))
        old_cell_share(last)
        activate(last, (GATE_F, GATE_O))
        tanh_of_cell(before)
        lay_memory(last)
        turn_cell(last)
        add_turned(last, "ig_t", closes=False)
        last["o_back"] = turn_back(nc, back_psum, last[GATE_O], ident, "o_back")
        forget_times_cell_turned(last)
        add_turned(last, "fc_t")
        hidden_product(before)
        new_cell_out(before)
        new_hidden(before)
        for part in halves:
            tanh_of_sum(last, part)
        cell_out_of_sum(last)
        for part in halves:
            hidden_product(last, part)
        for part in halves:
            new_hidden(last, part)
